import numpy as np
import ml_dtypes


def mxq(x, axis, fmt="e4m3"):
    dtype, down = {"e4m3": (ml_dtypes.float8_e4m3fn, 7), "e5m2": (ml_dtypes.float8_e5m2, 14)}[fmt]
    v = np.moveaxis(np.asarray(x, np.float32).astype(ml_dtypes.bfloat16).astype(np.float64), axis, -1)
    blocks = v.reshape(v.shape[:-1] + (-1, 32))
    amax = np.abs(blocks).max(-1, keepdims=True)
    byte = np.maximum(np.where(amax > 0, np.frexp(amax)[1] - 1 + 127, 0) - down, 1)
    scale = np.exp2(byte - 127.0)
    codes = (blocks / scale).astype(np.float32).astype(dtype).astype(np.float64)
    return np.moveaxis((codes * scale).reshape(v.shape), -1, axis)


WIDE = False


def mx_kscale(k):
    if not WIDE:
        return np.ones(k)
    levels = np.array([10, -10, 5, -5, 0])
    if k % 512:
        return np.exp2(np.random.permutation(np.resize(levels, k // 32))).repeat(32)
    a = np.empty((k // 512, 16))
    for p in range(k // 512):
        a[p, :8] = np.random.permutation(np.resize(levels, 8))
        for g in range(8):
            far = levels[np.abs(levels - a[p, g]) >= 10]
            a[p, g + 8] = far[np.random.randint(len(far))]
    return np.exp2(a.ravel()).repeat(32)


BF16 = ml_dtypes.bfloat16


def bf(x):
    return np.asarray(x, np.float32).astype(BF16)


def f64(x):
    return np.asarray(x).astype(np.float64)


B, N_I, N_H1, N_H2, N_H3, N_H4 = 512, 1024, 1024, 1024, 2048, 1024
K1 = N_I + N_H1


def sigmoid(v):
    return 1.0 / (1.0 + np.exp(-v))


def setup_inputs():
    s = mx_kscale(K1)

    def w(gain):
        return bf(np.random.standard_normal((N_H1, K1)) * gain / np.sqrt(K1) / s[None, :])

    def b():
        return bf(np.random.standard_normal(N_H1) * 0.3)

    return {"X": bf(np.random.standard_normal((B, N_I)) * s[:N_I]),
            "hidden1": bf(np.random.standard_normal((B, N_H1)) * s[N_I:]),
            "cell1": bf(np.random.standard_normal((B, N_H1))),
            "Wf1": w(1.0), "bf1": b(), "Wi1": w(1.0), "bi1": b(),
            "Wc1": w(5.0 / 3.0), "bc1": b(), "Wo1": w(1.0), "bo1": b()}


def reference(X, hidden1, cell1, Wf1, bf1, Wi1, bi1, Wc1, bc1, Wo1, bo1):
    zq = mxq(np.concatenate([f64(X), f64(hidden1)], axis=1), 1, "e4m3")
    f = sigmoid((zq @ mxq(f64(Wf1), 1, "e4m3").T) + f64(bf1))
    i = sigmoid((zq @ mxq(f64(Wi1), 1, "e4m3").T) + f64(bi1))
    cand = np.tanh((zq @ mxq(f64(Wc1), 1, "e4m3").T) + f64(bc1))
    o = sigmoid((zq @ mxq(f64(Wo1), 1, "e4m3").T) + f64(bo1))
    h_new = o * np.tanh(cand)
    c_new = f * f64(cell1) + cand * i
    return h_new, c_new

@@ -1,0 +1,288 @@
+from contextlib import ExitStack
+
+import concourse.mybir as mybir
+from concourse.masks import make_identity
+
+FP8X4 = mybir.dt.float8_e4m3fn_x4
+BF16 = mybir.dt.bfloat16
+F32 = mybir.dt.float32
+U32 = mybir.dt.uint32
+U8 = mybir.dt.uint8
+ACT = mybir.ActivationFunctionType
+ALU = mybir.AluOpType
+
+P = 128
+BATCH = 512
+N_IN = 1024
+N_HID = 1024
+K = N_IN + N_HID
+PACK = 4
+K_PASS = P * PACK
+PASSES = K // K_PASS
+BANK = 512
+
+SLAB_ROWS = 256
+ROW_TILES = SLAB_ROWS // P
+SLAB_WORDS = PASSES * SLAB_ROWS
+Z_SLABS = BATCH // SLAB_ROWS
+CHUNKS = N_HID // SLAB_ROWS
+GATES = ("c", "i", "f", "o")
+W_SLABS = CHUNKS * len(GATES)
+RAW_BUFS = 8
+QUANT_CALLS = 2
+
+FLOPS = 2 * BATCH * len(GATES) * N_HID * K
+
+
+def tile_quest_pa_kernel(
+    tc, X, hidden1, cell1, Wf1, bf1, Wi1, bi1, Wc1, bc1, Wo1, bo1, out_0, out_1
+):
+    nc = tc.nc
+    weight = {"f": Wf1, "i": Wi1, "c": Wc1, "o": Wo1}
+    bias = {"f": bf1, "i": bi1, "c": bc1, "o": bo1}
+    h_rows = out_0.rearrange("(t p) n -> p t n", p=P)
+    c_rows = out_1.rearrange("(t p) n -> p t n", p=P)
+
+    with ExitStack() as ctx:
+        const = ctx.enter_context(tc.tile_pool(name="const", bufs=1))
+        raw_pool = ctx.enter_context(tc.tile_pool(name="raw", bufs=RAW_BUFS))
+        grouped_pool = ctx.enter_context(tc.tile_pool(name="grouped", bufs=2))
+        w_pool = ctx.enter_context(tc.tile_pool(name="w_mx", bufs=3))
+        gate_pool = ctx.enter_context(tc.tile_pool(name="gates", bufs=2))
+        turn_pool = ctx.enter_context(tc.psum_pool(name="turned", bufs=4))
+        acc_pool = ctx.enter_context(tc.psum_pool(name="acc", bufs=4))
+        ctx.enter_context(tc.manual_schedule())
+
+        def load_slab(q):
+            raw = raw_pool.tile([P, ROW_TILES * K], BF16, name="raw", tag="raw")
+            raw_rows = raw[:].rearrange("p (a k) -> p a k", a=ROW_TILES)
+            if q < Z_SLABS:
+                rows = slice(q * SLAB_ROWS, (q + 1) * SLAB_ROWS)
+                nc.sync.dma_start(
+                    out=raw_rows[:, :, 0:N_IN],
+                    in_=X[rows, :].rearrange("(a p) k -> p a k", p=P),
+                )
+                nc.sync.dma_start(
+                    out=raw_rows[:, :, N_IN:K],
+                    in_=hidden1[rows, :].rearrange("(a p) k -> p a k", p=P),
+                )
+            else:
+                chunk, gate = divmod(q - Z_SLABS, len(GATES))
+                rows = slice(chunk * SLAB_ROWS, (chunk + 1) * SLAB_ROWS)
+                nc.sync.dma_start(
+                    out=raw_rows,
+                    in_=weight[GATES[gate]][rows, :].rearrange("(a p) k -> p a k", p=P),
+                )
+            return raw
+
+        def turn_slab(raw):
+            raw_words = raw[:].bitcast(F32)
+            grouped = grouped_pool.tile(
+                [P, SLAB_WORDS * PACK], BF16, name="grouped", tag="grouped", align_bytes=64
+            )
+            grouped_words = grouped[:].bitcast(F32)
+            for g in range(PASSES):
+                turned = turn_pool.tile([P, BANK], F32, name="turned", tag="turned")
+                for a in range(ROW_TILES):
+                    for u in range(2):
+                        first = a * (K // 2) + g * (K_PASS // 2) + u
+                        place = (2 * a + u) * P
+                        nc.tensor.transpose(
+                            turned[:, place : place + P],
+                            raw_words[:, first : first + 2 * P - 1 : 2],
+                            ident[:],
+                        )
+                nc.scalar.copy(
+                    out=grouped_words[:, g * BANK : (g + 1) * BANK].rearrange(
+                        "p (a r u) -> p a r u", a=ROW_TILES, u=2
+                    ),
+                    in_=turned[:].rearrange("p (a u r) -> p a r u", a=ROW_TILES, u=2),
+                )
+            return grouped
+
+        def quantise_slab(grouped, codes, scales):
+            words = SLAB_WORDS // QUANT_CALLS
+            for call in range(QUANT_CALLS):
+                nc.vector.quantize_mx(
+                    out=codes[:, call * words : (call + 1) * words].bitcast(FP8X4),
+                    scales=scales[:, call * words : (call + 1) * words],
+                    in_=grouped[:, call * words * PACK : (call + 1) * words * PACK],
+                )
+
+        def spread_bias(gate):
+            for half in range(N_HID // BANK):
+                cols = slice(gate * N_HID + half * BANK, gate * N_HID + (half + 1) * BANK)
+                spread = acc_pool.tile([P, BANK], F32, name="spread", tag="acc")
+                nc.tensor.matmul(
+                    out=spread[:], lhsT=ones[:], rhs=bias_rows[:, cols], start=True, stop=True
+                )
+                nc.vector.tensor_copy(out=bias_all[:, cols], in_=spread[:])
+
+        def multiply_slab(codes, scales):
+            banks = []
+            for pair in range(Z_SLABS):
+                acc = acc_pool.tile([P, BANK], F32, name="acc", tag="acc")
+                for a in range(ROW_TILES):
+                    for g in range(PASSES):
+                        z_cols = slice(g * SLAB_ROWS + a * P, g * SLAB_ROWS + (a + 1) * P)
+                        w_cols = slice(g * SLAB_ROWS, (g + 1) * SLAB_ROWS)
+                        nc.tensor.matmul_mx(
+                            out=acc[:, a * SLAB_ROWS : (a + 1) * SLAB_ROWS],
+                            lhsT=z_codes[pair][:, z_cols].bitcast(FP8X4),
+                            lhsT_scale=z_scales[pair][:, z_cols],
+                            rhs=codes[:, w_cols].bitcast(FP8X4),
+                            rhs_scale=scales[:, w_cols],
+                            start=(g == 0),
+                            stop=(g == PASSES - 1),
+                        )
+                banks.append(acc)
+            return banks
+
+        def add_bias(s, banks):
+            chunk, gate = divmod(s, len(GATES))
+            first = gate * N_HID + chunk * SLAB_ROWS
+            value = gate_pool.tile(
+                [P, Z_SLABS * BANK], F32, name="gate_" + GATES[gate], tag="gate_" + GATES[gate]
+            )
+            for pair in range(Z_SLABS):
+                nc.vector.tensor_tensor(
+                    out=value[:, pair * BANK : (pair + 1) * BANK].rearrange(
+                        "p (a n) -> p a n", a=ROW_TILES
+                    ),
+                    in0=banks[pair][:].rearrange("p (a n) -> p a n", a=ROW_TILES),
+                    in1=bias_all[:, first : first + SLAB_ROWS]
+                    .unsqueeze(1)
+                    .to_broadcast([P, ROW_TILES, SLAB_ROWS]),
+                    op=ALU.add,
+                )
+            return value
+
+        def activate(s, value):
+            gate = GATES[s % len(GATES)]
+            for pair in range(Z_SLABS):
+                cols = slice(pair * BANK, (pair + 1) * BANK)
+                nc.scalar.activation(
+                    out=value[:, cols],
+                    in_=value[:, cols],
+                    func=ACT.Tanh if gate == "c" else ACT.Sigmoid,
+                )
+            if gate != "c":
+                return None
+            squashed = gate_pool.tile([P, Z_SLABS * BANK], F32, name="squashed", tag="squashed")
+            for pair in range(Z_SLABS):
+                cols = slice(pair * BANK, (pair + 1) * BANK)
+                nc.scalar.activation(out=squashed[:, cols], in_=value[:, cols], func=ACT.Tanh)
+            return squashed
+
+        def combine(step):
+            chunk, kind = divmod(step, 4)
+            out_cols = slice(chunk * SLAB_ROWS, (chunk + 1) * SLAB_ROWS)
+            for pair in range(Z_SLABS):
+                cols = slice(pair * BANK, (pair + 1) * BANK)
+                tiles = slice(pair * ROW_TILES, (pair + 1) * ROW_TILES)
+                if kind == 0:
+                    nc.vector.tensor_tensor(
+                        out=values[chunk, "i"][:, cols],
+                        in0=values[chunk, "i"][:, cols],
+                        in1=values[chunk, "c"][:, cols],
+                        op=ALU.mult,
+                    )
+                elif kind == 1:
+                    nc.vector.tensor_tensor(
+                        out=values[chunk, "f"][:, cols].rearrange("p (a n) -> p a n", a=ROW_TILES),
+                        in0=values[chunk, "f"][:, cols].rearrange("p (a n) -> p a n", a=ROW_TILES),
+                        in1=cell_rows[:, tiles, out_cols],
+                        op=ALU.mult,
+                    )
+                elif kind == 2:
+                    nc.vector.tensor_tensor(
+                        out=values[chunk, "f"][:, cols],
+                        in0=values[chunk, "f"][:, cols],
+                        in1=values[chunk, "i"][:, cols],
+                        op=ALU.add,
+                    )
+                    nc.sync.dma_start(
+                        out=c_rows[:, tiles, out_cols],
+                        in_=values[chunk, "f"][:, cols].rearrange("p (a n) -> p a n", a=ROW_TILES),
+                    )
+                else:
+                    nc.vector.tensor_tensor(
+                        out=values[chunk, "o"][:, cols],
+                        in0=values[chunk, "o"][:, cols],
+                        in1=values[chunk, "tanh_c"][:, cols],
+                        op=ALU.mult,
+                    )
+                    nc.sync.dma_start(
+                        out=h_rows[:, tiles, out_cols],
+                        in_=values[chunk, "o"][:, cols].rearrange("p (a n) -> p a n", a=ROW_TILES),
+                    )
+
+        raws = {}
+        for q in range(RAW_BUFS):
+            raws[q] = load_slab(q)
+        cell_sb = const.tile([P, (BATCH // P) * N_HID], BF16, name="cell_sb")
+        cell_rows = cell_sb[:].rearrange("p (t n) -> p t n", n=N_HID)
+        nc.sync.dma_start(out=cell_rows, in_=cell1.rearrange("(t p) n -> p t n", p=P))
+
+        ident = const.tile([P, P], F32, name="ident")
+        make_identity(nc, ident[:])
+        ones = const.tile([P, P], BF16, name="ones")
+        nc.vector.memset(ones[:], 1.0)
+        bias_rows = const.tile([P, len(GATES) * N_HID], BF16, name="bias_rows")
+        nc.vector.memset(bias_rows[:].bitcast(F32), 0.0)
+        for gate in range(len(GATES)):
+            nc.scalar.dma_start(
+                out=bias_rows[0:1, gate * N_HID : (gate + 1) * N_HID],
+                in_=bias[GATES[gate]].rearrange("(o n) -> o n", o=1),
+            )
+        bias_all = const.tile([P, len(GATES) * N_HID], F32, name="bias_all")
+        warm = const.tile([P, 1], F32, name="warm")
+        nc.vector.memset(warm[:], 0.0)
+        nc.scalar.activation(out=warm[:], in_=warm[:], func=ACT.Sigmoid)
+
+        z_codes = []
+        z_scales = []
+        for pair in range(Z_SLABS):
+            z_codes.append(
+                const.tile([P, SLAB_WORDS], U32, name="z_codes%d" % pair, align_bytes=64)
+            )
+            z_scales.append(
+                const.tile([P, SLAB_WORDS], U8, name="z_scales%d" % pair, align_bytes=64)
+            )
+
+        mx = {}
+        sums = {}
+        values = {}
+        next_step = 0
+        for s in range(-Z_SLABS - 1, W_SLABS + 1):
+            turning = s + 1 < W_SLABS
+            if turning:
+                q = s + 1 + Z_SLABS
+                grouped = turn_slab(raws[q])
+                if q + RAW_BUFS < Z_SLABS + W_SLABS:
+                    raws[q + RAW_BUFS] = load_slab(q + RAW_BUFS)
+            if s < len(GATES) - Z_SLABS - 1:
+                spread_bias(s + Z_SLABS + 1)
+            if s >= 3:
+                combine(next_step)
+                next_step += 1
+            if 0 <= s - 1:
+                chunk, gate = divmod(s - 1, len(GATES))
+                values[chunk, GATES[gate]] = add_bias(s - 1, sums[s - 1])
+                squashed = activate(s - 1, values[chunk, GATES[gate]])
+                if squashed is not None:
+                    values[chunk, "tanh_c"] = squashed
+            if turning:
+                if s + 1 < 0:
+                    codes, scales = z_codes[s + 1 + Z_SLABS], z_scales[s + 1 + Z_SLABS]
+                else:
+                    codes = w_pool.tile([P, SLAB_WORDS], U32, name="codes", tag="codes", align_bytes=64)
+                    scales = w_pool.tile([P, SLAB_WORDS], U8, name="scales", tag="scales", align_bytes=64)
+                    mx[s + 1] = (codes, scales)
+                quantise_slab(grouped, codes, scales)
+            else:
+                combine(next_step)
+                next_step += 1
+            if 0 <= s < W_SLABS:
+                codes, scales = mx[s]
+                sums[s] = multiply_slab(codes, scales)

@@ -28,8 +28,12 @@ Z_SLABS = BATCH // SLAB_ROWS
 CHUNKS = N_HID // SLAB_ROWS
 GATES = ("c", "i", "f", "o")
 W_SLABS = CHUNKS * len(GATES)
+LAST = W_SLABS - 1
 RAW_BUFS = 8
 QUANT_CALLS = 2
+
+SORTED = (3, 2)
+FIRST_SORTED = 2
 
 FLOPS = 2 * BATCH * len(GATES) * N_HID * K
 
@@ -46,6 +50,7 @@ def tile_quest_pa_kernel(
     with ExitStack() as ctx:
         const = ctx.enter_context(tc.tile_pool(name="const", bufs=1))
         raw_pool = ctx.enter_context(tc.tile_pool(name="raw", bufs=RAW_BUFS))
+        sorted_pool = ctx.enter_context(tc.tile_pool(name="sorted", bufs=2))
         grouped_pool = ctx.enter_context(tc.tile_pool(name="grouped", bufs=2))
         w_pool = ctx.enter_context(tc.tile_pool(name="w_mx", bufs=3))
         gate_pool = ctx.enter_context(tc.tile_pool(name="gates", bufs=2))
@@ -53,11 +58,12 @@ def tile_quest_pa_kernel(
         acc_pool = ctx.enter_context(tc.psum_pool(name="acc", bufs=4))
         ctx.enter_context(tc.manual_schedule())
 
-        def load_slab(q):
+        def load_slab(slab):
+            kind, index = slab
             raw = raw_pool.tile([P, ROW_TILES * K], BF16, name="raw", tag="raw")
             raw_rows = raw[:].rearrange("p (a k) -> p a k", a=ROW_TILES)
-            if q < Z_SLABS:
-                rows = slice(q * SLAB_ROWS, (q + 1) * SLAB_ROWS)
+            if kind == "z":
+                rows = slice(index * SLAB_ROWS, (index + 1) * SLAB_ROWS)
                 nc.sync.dma_start(
                     out=raw_rows[:, :, 0:N_IN],
                     in_=X[rows, :].rearrange("(a p) k -> p a k", p=P),
@@ -67,7 +73,7 @@ def tile_quest_pa_kernel(
                     in_=hidden1[rows, :].rearrange("(a p) k -> p a k", p=P),
                 )
             else:
-                chunk, gate = divmod(q - Z_SLABS, len(GATES))
+                chunk, gate = divmod(index, len(GATES))
                 rows = slice(chunk * SLAB_ROWS, (chunk + 1) * SLAB_ROWS)
                 nc.sync.dma_start(
                     out=raw_rows,
@@ -75,7 +81,21 @@ def tile_quest_pa_kernel(
                 )
             return raw
 
-        def turn_slab(raw):
+        def sort_slab(raw):
+            in_order = []
+            for a in range(ROW_TILES):
+                words = SORTED[a] * K_PASS // 2
+                tile = sorted_pool.tile([P, words], F32, name="in_order%d" % a, tag="in_order%d" % a)
+                nc.vector.tensor_copy(
+                    out=tile[:].rearrange("p (u w) -> p u w", u=2),
+                    in_=raw[:]
+                    .bitcast(F32)[:, a * (K // 2) : a * (K // 2) + words]
+                    .rearrange("p (w u) -> p u w", u=2),
+                )
+                in_order.append(tile)
+            return in_order
+
+        def turn_slab(raw, in_order):
             raw_words = raw[:].bitcast(F32)
             grouped = grouped_pool.tile(
                 [P, SLAB_WORDS * PACK], BF16, name="grouped", tag="grouped", align_bytes=64
@@ -85,13 +105,14 @@ def tile_quest_pa_kernel(
                 turned = turn_pool.tile([P, BANK], F32, name="turned", tag="turned")
                 for a in range(ROW_TILES):
                     for u in range(2):
-                        first = a * (K // 2) + g * (K_PASS // 2) + u
                         place = (2 * a + u) * P
-                        nc.tensor.transpose(
-                            turned[:, place : place + P],
-                            raw_words[:, first : first + 2 * P - 1 : 2],
-                            ident[:],
-                        )
+                        if in_order is not None and g < SORTED[a]:
+                            first = (u * SORTED[a] + g) * P
+                            words = in_order[a][:, first : first + P]
+                        else:
+                            first = a * (K // 2) + g * (K_PASS // 2) + u
+                            words = raw_words[:, first : first + 2 * P - 1 : 2]
+                        nc.tensor.transpose(turned[:, place : place + P], words, ident[:])
                 nc.scalar.copy(
                     out=grouped_words[:, g * BANK : (g + 1) * BANK].rearrange(
                         "p (a r u) -> p a r u", a=ROW_TILES, u=2
@@ -110,179 +131,193 @@ def tile_quest_pa_kernel(
                 )
 
         def spread_bias(gate):
+            spread = acc_pool.tile([P, N_HID], BF16, name="spread", tag="acc")
             for half in range(N_HID // BANK):
-                cols = slice(gate * N_HID + half * BANK, gate * N_HID + (half + 1) * BANK)
-                spread = acc_pool.tile([P, BANK], F32, name="spread", tag="acc")
+                cols = slice(half * BANK, (half + 1) * BANK)
                 nc.tensor.matmul(
-                    out=spread[:], lhsT=ones[:], rhs=bias_rows[:, cols], start=True, stop=True
+                    out=spread[:, cols],
+                    lhsT=ident_bf[:, gate : gate + 1].to_broadcast([P, P]),
+                    rhs=bias_rows[:, cols],
+                    start=True,
+                    stop=True,
                 )
-                nc.vector.tensor_copy(out=bias_all[:, cols], in_=spread[:])
+            nc.vector.tensor_copy(out=bias_all[:, gate * N_HID : (gate + 1) * N_HID], in_=spread[:])
 
-        def multiply_slab(codes, scales):
-            banks = []
-            for pair in range(Z_SLABS):
-                acc = acc_pool.tile([P, BANK], F32, name="acc", tag="acc")
-                for a in range(ROW_TILES):
-                    for g in range(PASSES):
-                        z_cols = slice(g * SLAB_ROWS + a * P, g * SLAB_ROWS + (a + 1) * P)
-                        w_cols = slice(g * SLAB_ROWS, (g + 1) * SLAB_ROWS)
-                        nc.tensor.matmul_mx(
-                            out=acc[:, a * SLAB_ROWS : (a + 1) * SLAB_ROWS],
-                            lhsT=z_codes[pair][:, z_cols].bitcast(FP8X4),
-                            lhsT_scale=z_scales[pair][:, z_cols],
-                            rhs=codes[:, w_cols].bitcast(FP8X4),
-                            rhs_scale=scales[:, w_cols],
-                            start=(g == 0),
-                            stop=(g == PASSES - 1),
-                        )
-                banks.append(acc)
-            return banks
+        def multiply(s, pair):
+            codes, scales = mx[s]
+            acc = acc_pool.tile([P, BANK], F32, name="acc", tag="acc")
+            for a in range(ROW_TILES):
+                for g in range(PASSES):
+                    z_cols = slice(g * SLAB_ROWS + a * P, g * SLAB_ROWS + (a + 1) * P)
+                    w_cols = slice(g * SLAB_ROWS, (g + 1) * SLAB_ROWS)
+                    nc.tensor.matmul_mx(
+                        out=acc[:, a * SLAB_ROWS : (a + 1) * SLAB_ROWS],
+                        lhsT=z_mx[pair][0][:, z_cols].bitcast(FP8X4),
+                        lhsT_scale=z_mx[pair][1][:, z_cols],
+                        rhs=codes[:, w_cols].bitcast(FP8X4),
+                        rhs_scale=scales[:, w_cols],
+                        start=(g == 0),
+                        stop=(g == PASSES - 1),
+                    )
+            sums[s, pair] = acc
 
-        def add_bias(s, banks):
+        def half_of(pair):
+            return slice(pair * BANK, (pair + 1) * BANK)
+
+        def finish(s, pair):
             chunk, gate = divmod(s, len(GATES))
+            name = GATES[gate]
+            if pair == 0:
+                values[chunk, name] = gate_pool.tile(
+                    [P, Z_SLABS * BANK], F32, name="gate_" + name, tag="gate_" + name
+                )
+                if name == "c":
+                    values[chunk, "tanh_c"] = gate_pool.tile(
+                        [P, Z_SLABS * BANK], F32, name="tanh_c", tag="tanh_c"
+                    )
+            value = values[chunk, name][:, half_of(pair)]
             first = gate * N_HID + chunk * SLAB_ROWS
-            value = gate_pool.tile(
-                [P, Z_SLABS * BANK], F32, name="gate_" + GATES[gate], tag="gate_" + GATES[gate]
+            nc.vector.tensor_tensor(
+                out=value.rearrange("p (a n) -> p a n", a=ROW_TILES),
+                in0=sums[s, pair][:].rearrange("p (a n) -> p a n", a=ROW_TILES),
+                in1=bias_all[:, first : first + SLAB_ROWS]
+                .unsqueeze(1)
+                .to_broadcast([P, ROW_TILES, SLAB_ROWS]),
+                op=ALU.add,
             )
-            for pair in range(Z_SLABS):
+            nc.scalar.activation(
+                out=value, in_=value, func=ACT.Tanh if name == "c" else ACT.Sigmoid
+            )
+            if name == "c":
+                nc.scalar.activation(
+                    out=values[chunk, "tanh_c"][:, half_of(pair)], in_=value, func=ACT.Tanh
+                )
+
+        def combine(chunk, kind, pairs):
+            cols = slice(pairs[0] * BANK, (pairs[-1] + 1) * BANK)
+            tiles = slice(pairs[0] * ROW_TILES, (pairs[-1] + 1) * ROW_TILES)
+            out_cols = slice(chunk * SLAB_ROWS, (chunk + 1) * SLAB_ROWS)
+
+            def by_tile(name):
+                return values[chunk, name][:, cols].rearrange("p (t n) -> p t n", n=SLAB_ROWS)
+
+            if kind == "cand * i":
                 nc.vector.tensor_tensor(
-                    out=value[:, pair * BANK : (pair + 1) * BANK].rearrange(
-                        "p (a n) -> p a n", a=ROW_TILES
-                    ),
-                    in0=banks[pair][:].rearrange("p (a n) -> p a n", a=ROW_TILES),
-                    in1=bias_all[:, first : first + SLAB_ROWS]
-                    .unsqueeze(1)
-                    .to_broadcast([P, ROW_TILES, SLAB_ROWS]),
+                    out=values[chunk, "i"][:, cols],
+                    in0=values[chunk, "i"][:, cols],
+                    in1=values[chunk, "c"][:, cols],
+                    op=ALU.mult,
+                )
+            elif kind == "f * cell":
+                nc.vector.tensor_tensor(
+                    out=by_tile("f"),
+                    in0=by_tile("f"),
+                    in1=cell_rows[:, tiles, out_cols],
+                    op=ALU.mult,
+                )
+            elif kind == "c_new":
+                nc.vector.tensor_tensor(
+                    out=values[chunk, "f"][:, cols],
+                    in0=values[chunk, "f"][:, cols],
+                    in1=values[chunk, "i"][:, cols],
                     op=ALU.add,
                 )
-            return value
-
-        def activate(s, value):
-            gate = GATES[s % len(GATES)]
-            for pair in range(Z_SLABS):
-                cols = slice(pair * BANK, (pair + 1) * BANK)
-                nc.scalar.activation(
-                    out=value[:, cols],
-                    in_=value[:, cols],
-                    func=ACT.Tanh if gate == "c" else ACT.Sigmoid,
+                nc.sync.dma_start(out=c_rows[:, tiles, out_cols], in_=by_tile("f"))
+            else:
+                nc.vector.tensor_tensor(
+                    out=values[chunk, "o"][:, cols],
+                    in0=values[chunk, "o"][:, cols],
+                    in1=values[chunk, "tanh_c"][:, cols],
+                    op=ALU.mult,
                 )
-            if gate != "c":
-                return None
-            squashed = gate_pool.tile([P, Z_SLABS * BANK], F32, name="squashed", tag="squashed")
-            for pair in range(Z_SLABS):
-                cols = slice(pair * BANK, (pair + 1) * BANK)
-                nc.scalar.activation(out=squashed[:, cols], in_=value[:, cols], func=ACT.Tanh)
-            return squashed
+                nc.sync.dma_start(out=h_rows[:, tiles, out_cols], in_=by_tile("o"))
 
-        def combine(step):
-            chunk, kind = divmod(step, 4)
-            out_cols = slice(chunk * SLAB_ROWS, (chunk + 1) * SLAB_ROWS)
-            for pair in range(Z_SLABS):
-                cols = slice(pair * BANK, (pair + 1) * BANK)
-                tiles = slice(pair * ROW_TILES, (pair + 1) * ROW_TILES)
-                if kind == 0:
-                    nc.vector.tensor_tensor(
-                        out=values[chunk, "i"][:, cols],
-                        in0=values[chunk, "i"][:, cols],
-                        in1=values[chunk, "c"][:, cols],
-                        op=ALU.mult,
-                    )
-                elif kind == 1:
-                    nc.vector.tensor_tensor(
-                        out=values[chunk, "f"][:, cols].rearrange("p (a n) -> p a n", a=ROW_TILES),
-                        in0=values[chunk, "f"][:, cols].rearrange("p (a n) -> p a n", a=ROW_TILES),
-                        in1=cell_rows[:, tiles, out_cols],
-                        op=ALU.mult,
-                    )
-                elif kind == 2:
-                    nc.vector.tensor_tensor(
-                        out=values[chunk, "f"][:, cols],
-                        in0=values[chunk, "f"][:, cols],
-                        in1=values[chunk, "i"][:, cols],
-                        op=ALU.add,
-                    )
-                    nc.sync.dma_start(
-                        out=c_rows[:, tiles, out_cols],
-                        in_=values[chunk, "f"][:, cols].rearrange("p (a n) -> p a n", a=ROW_TILES),
-                    )
-                else:
-                    nc.vector.tensor_tensor(
-                        out=values[chunk, "o"][:, cols],
-                        in0=values[chunk, "o"][:, cols],
-                        in1=values[chunk, "tanh_c"][:, cols],
-                        op=ALU.mult,
-                    )
-                    nc.sync.dma_start(
-                        out=h_rows[:, tiles, out_cols],
-                        in_=values[chunk, "o"][:, cols].rearrange("p (a n) -> p a n", a=ROW_TILES),
-                    )
-
+        order = [("z", 0), ("w", 0), ("z", 1)] + [("w", s) for s in range(1, W_SLABS)]
         raws = {}
-        for q in range(RAW_BUFS):
-            raws[q] = load_slab(q)
+        for slab in order[:RAW_BUFS]:
+            raws[slab] = load_slab(slab)
         cell_sb = const.tile([P, (BATCH // P) * N_HID], BF16, name="cell_sb")
         cell_rows = cell_sb[:].rearrange("p (t n) -> p t n", n=N_HID)
         nc.sync.dma_start(out=cell_rows, in_=cell1.rearrange("(t p) n -> p t n", p=P))
 
-        ident = const.tile([P, P], F32, name="ident")
-        make_identity(nc, ident[:])
-        ones = const.tile([P, P], BF16, name="ones")
-        nc.vector.memset(ones[:], 1.0)
-        bias_rows = const.tile([P, len(GATES) * N_HID], BF16, name="bias_rows")
+        bias_rows = const.tile([P, N_HID], BF16, name="bias_rows")
         nc.vector.memset(bias_rows[:].bitcast(F32), 0.0)
         for gate in range(len(GATES)):
             nc.scalar.dma_start(
-                out=bias_rows[0:1, gate * N_HID : (gate + 1) * N_HID],
+                out=bias_rows[gate : gate + 1, :],
                 in_=bias[GATES[gate]].rearrange("(o n) -> o n", o=1),
             )
-        bias_all = const.tile([P, len(GATES) * N_HID], F32, name="bias_all")
+        ident = const.tile([P, P], F32, name="ident")
+        make_identity(nc, ident[:])
+        ident_bf = const.tile([P, P], BF16, name="ident_bf")
+        nc.vector.tensor_copy(out=ident_bf[:], in_=ident[:])
+        bias_all = const.tile([P, len(GATES) * N_HID], BF16, name="bias_all")
         warm = const.tile([P, 1], F32, name="warm")
         nc.vector.memset(warm[:], 0.0)
         nc.scalar.activation(out=warm[:], in_=warm[:], func=ACT.Sigmoid)
 
-        z_codes = []
-        z_scales = []
+        z_mx = []
         for pair in range(Z_SLABS):
-            z_codes.append(
-                const.tile([P, SLAB_WORDS], U32, name="z_codes%d" % pair, align_bytes=64)
+            z_mx.append(
+                (
+                    const.tile([P, SLAB_WORDS], U32, name="z_codes%d" % pair, align_bytes=64),
+                    const.tile([P, SLAB_WORDS], U8, name="z_scales%d" % pair, align_bytes=64),
+                )
             )
-            z_scales.append(
-                const.tile([P, SLAB_WORDS], U8, name="z_scales%d" % pair, align_bytes=64)
-            )
-
         mx = {}
         sums = {}
         values = {}
-        next_step = 0
-        for s in range(-Z_SLABS - 1, W_SLABS + 1):
-            turning = s + 1 < W_SLABS
-            if turning:
-                q = s + 1 + Z_SLABS
-                grouped = turn_slab(raws[q])
-                if q + RAW_BUFS < Z_SLABS + W_SLABS:
-                    raws[q + RAW_BUFS] = load_slab(q + RAW_BUFS)
-            if s < len(GATES) - Z_SLABS - 1:
-                spread_bias(s + Z_SLABS + 1)
-            if s >= 3:
-                combine(next_step)
-                next_step += 1
-            if 0 <= s - 1:
-                chunk, gate = divmod(s - 1, len(GATES))
-                values[chunk, GATES[gate]] = add_bias(s - 1, sums[s - 1])
-                squashed = activate(s - 1, values[chunk, GATES[gate]])
-                if squashed is not None:
-                    values[chunk, "tanh_c"] = squashed
-            if turning:
-                if s + 1 < 0:
-                    codes, scales = z_codes[s + 1 + Z_SLABS], z_scales[s + 1 + Z_SLABS]
-                else:
-                    codes = w_pool.tile([P, SLAB_WORDS], U32, name="codes", tag="codes", align_bytes=64)
-                    scales = w_pool.tile([P, SLAB_WORDS], U8, name="scales", tag="scales", align_bytes=64)
-                    mx[s + 1] = (codes, scales)
-                quantise_slab(grouped, codes, scales)
+
+        def turn(slab, in_order=None):
+            grouped = turn_slab(raws[slab], in_order)
+            ahead = order.index(slab) + RAW_BUFS
+            if ahead < len(order):
+                raws[order[ahead]] = load_slab(order[ahead])
+            return grouped
+
+        def quantise(slab, grouped):
+            kind, index = slab
+            if kind == "z":
+                codes, scales = z_mx[index]
             else:
-                combine(next_step)
-                next_step += 1
-            if 0 <= s < W_SLABS:
-                codes, scales = mx[s]
-                sums[s] = multiply_slab(codes, scales)
+                codes = w_pool.tile([P, SLAB_WORDS], U32, name="codes", tag="codes", align_bytes=64)
+                scales = w_pool.tile([P, SLAB_WORDS], U8, name="scales", tag="scales", align_bytes=64)
+                mx[index] = (codes, scales)
+            quantise_slab(grouped, codes, scales)
+
+        for gate, slab in enumerate(order[:4]):
+            grouped = turn(slab)
+            quantise(slab, grouped)
+            spread_bias(gate)
+            if gate >= 2:
+                multiply(0, gate - 2)
+
+        kinds = ("cand * i", "f * cell", "c_new", "h_new")
+        steps = [(chunk, kind) for chunk in range(CHUNKS) for kind in kinds]
+        pairs = (0, 1)
+        in_order = sort_slab(raws["w", FIRST_SORTED])
+        for s in range(1, LAST):
+            grouped = turn(("w", s + 1), in_order)
+            for pair in pairs:
+                finish(s - 1, pair)
+            if s >= 3:
+                combine(*steps[s - 3], pairs)
+            if s + 2 <= LAST:
+                in_order = sort_slab(raws["w", s + 2])
+            quantise(("w", s + 1), grouped)
+            for pair in pairs:
+                multiply(s, pair)
+
+        for pair in pairs:
+            finish(LAST - 1, pair)
+        for pair in pairs:
+            multiply(LAST, pair)
+        combine(CHUNKS - 1, "cand * i", pairs)
+        finish(LAST, 0)
+        combine(CHUNKS - 1, "f * cell", (0,))
+        combine(CHUNKS - 1, "f * cell", (1,))
+        finish(LAST, 1)
+        combine(CHUNKS - 1, "c_new", (0,))
+        combine(CHUNKS - 1, "h_new", (0,))
+        combine(CHUNKS - 1, "c_new", (1,))
+        combine(CHUNKS - 1, "h_new", (1,))

@@ -32,8 +32,12 @@ LAST = W_SLABS - 1
 RAW_BUFS = 8
 QUANT_CALLS = 2
 
-SORTED = (3, 2)
-FIRST_SORTED = 2
+SORTED = 3
+BLOCK_WORDS = 16
+RUN = BLOCK_WORDS // 2
+ROW_WORDS = K // 2
+SORTED_WORDS = SORTED * K_PASS // 2
+PASS_BLOCKS = K_PASS // 32
 
 FLOPS = 2 * BATCH * len(GATES) * N_HID * K
 
@@ -63,15 +67,10 @@ def tile_quest_pa_kernel(
             raw = raw_pool.tile([P, ROW_TILES * K], BF16, name="raw", tag="raw")
             raw_rows = raw[:].rearrange("p (a k) -> p a k", a=ROW_TILES)
             if kind == "z":
-                rows = slice(index * SLAB_ROWS, (index + 1) * SLAB_ROWS)
-                nc.sync.dma_start(
-                    out=raw_rows[:, :, 0:N_IN],
-                    in_=X[rows, :].rearrange("(a p) k -> p a k", p=P),
-                )
-                nc.sync.dma_start(
-                    out=raw_rows[:, :, N_IN:K],
-                    in_=hidden1[rows, :].rearrange("(a p) k -> p a k", p=P),
-                )
+                for source, cols in ((X, slice(0, N_IN)), (hidden1, slice(N_IN, K))):
+                    for a in range(ROW_TILES):
+                        first = index * SLAB_ROWS + a * P
+                        nc.sync.dma_start(out=raw_rows[:, a, cols], in_=source[first : first + P, :])
             else:
                 chunk, gate = divmod(index, len(GATES))
                 rows = slice(chunk * SLAB_ROWS, (chunk + 1) * SLAB_ROWS)
@@ -81,19 +80,28 @@ def tile_quest_pa_kernel(
                 )
             return raw
 
-        def sort_slab(raw):
-            in_order = []
-            for a in range(ROW_TILES):
-                words = SORTED[a] * K_PASS // 2
-                tile = sorted_pool.tile([P, words], F32, name="in_order%d" % a, tag="in_order%d" % a)
-                nc.vector.tensor_copy(
-                    out=tile[:].rearrange("p (u w) -> p u w", u=2),
-                    in_=raw[:]
-                    .bitcast(F32)[:, a * (K // 2) : a * (K // 2) + words]
-                    .rearrange("p (w u) -> p u w", u=2),
-                )
-                in_order.append(tile)
-            return in_order
+        def sort_words(slab, a, passes):
+            first = a * ROW_WORDS + passes[0] * (K_PASS // 2)
+            blocks = slice(passes[0] * PASS_BLOCKS, (passes[-1] + 1) * PASS_BLOCKS)
+            nc.vector.tensor_copy(
+                out=in_orders[slab][a][:].rearrange("p (u b i) -> p u b i", u=2, i=RUN)[:, :, blocks, :],
+                in_=raws[slab][:]
+                .bitcast(F32)[:, first : first + len(passes) * (K_PASS // 2)]
+                .rearrange("p (b u i) -> p u b i", u=2, i=RUN),
+            )
+
+        def sort_slab(slab):
+            in_orders[slab] = [
+                sorted_pool.tile([P, SORTED_WORDS], F32, name="in_order%d" % a, tag="in_order%d" % a)
+                for a in range(ROW_TILES)
+            ]
+            if slab[0] == "z":
+                for passes in (range(0, 2), range(2, SORTED)):
+                    for a in range(ROW_TILES):
+                        sort_words(slab, a, passes)
+            else:
+                for a in range(ROW_TILES):
+                    sort_words(slab, a, range(SORTED))
 
         def turn_slab(raw, in_order):
             raw_words = raw[:].bitcast(F32)
@@ -106,11 +114,11 @@ def tile_quest_pa_kernel(
                 for a in range(ROW_TILES):
                     for u in range(2):
                         place = (2 * a + u) * P
-                        if in_order is not None and g < SORTED[a]:
-                            first = (u * SORTED[a] + g) * P
+                        if g < SORTED:
+                            first = (u * SORTED + g) * P
                             words = in_order[a][:, first : first + P]
                         else:
-                            first = a * (K // 2) + g * (K_PASS // 2) + u
+                            first = a * ROW_WORDS + g * (K_PASS // 2) + u
                             words = raw_words[:, first : first + 2 * P - 1 : 2]
                         nc.tensor.transpose(turned[:, place : place + P], words, ident[:])
                 nc.scalar.copy(
@@ -161,76 +169,70 @@ def tile_quest_pa_kernel(
                     )
             sums[s, pair] = acc
 
-        def half_of(pair):
-            return slice(pair * BANK, (pair + 1) * BANK)
-
-        def finish(s, pair):
+        def add_bias(s, pair):
             chunk, gate = divmod(s, len(GATES))
             name = GATES[gate]
             if pair == 0:
                 values[chunk, name] = gate_pool.tile(
                     [P, Z_SLABS * BANK], F32, name="gate_" + name, tag="gate_" + name
                 )
-                if name == "c":
-                    values[chunk, "tanh_c"] = gate_pool.tile(
-                        [P, Z_SLABS * BANK], F32, name="tanh_c", tag="tanh_c"
-                    )
-            value = values[chunk, name][:, half_of(pair)]
             first = gate * N_HID + chunk * SLAB_ROWS
             nc.vector.tensor_tensor(
-                out=value.rearrange("p (a n) -> p a n", a=ROW_TILES),
-                in0=sums[s, pair][:].rearrange("p (a n) -> p a n", a=ROW_TILES),
+                out=half(chunk, name, pair, by_tile=True),
+                in0=sums[s, pair][:].rearrange("p (t n) -> p t n", n=SLAB_ROWS),
                 in1=bias_all[:, first : first + SLAB_ROWS]
                 .unsqueeze(1)
                 .to_broadcast([P, ROW_TILES, SLAB_ROWS]),
                 op=ALU.add,
             )
-            nc.scalar.activation(
-                out=value, in_=value, func=ACT.Tanh if name == "c" else ACT.Sigmoid
-            )
-            if name == "c":
-                nc.scalar.activation(
-                    out=values[chunk, "tanh_c"][:, half_of(pair)], in_=value, func=ACT.Tanh
-                )
 
-        def combine(chunk, kind, pairs):
-            cols = slice(pairs[0] * BANK, (pairs[-1] + 1) * BANK)
-            tiles = slice(pairs[0] * ROW_TILES, (pairs[-1] + 1) * ROW_TILES)
+        def activate(s, pair):
+            chunk, gate = divmod(s, len(GATES))
+            value = half(chunk, GATES[gate], pair)
+            nc.scalar.activation(
+                out=value, in_=value, func=ACT.Tanh if GATES[gate] == "c" else ACT.Sigmoid
+            )
+
+        def squash(chunk, pair):
+            if pair == 0:
+                values[chunk, "t"] = gate_pool.tile(
+                    [P, Z_SLABS * BANK], F32, name="t", tag="t"
+                )
+            nc.scalar.activation(
+                out=half(chunk, "t", pair), in_=half(chunk, "c", pair), func=ACT.Tanh
+            )
+
+        def half(chunk, name, place, by_tile=False):
+            view = values[chunk, name][:, place * BANK : (place + 1) * BANK]
+            return view.rearrange("p (t n) -> p t n", n=SLAB_ROWS) if by_tile else view
+
+        def combine(engine, chunk, kind, pair, places):
+            tiles = slice(pair * ROW_TILES, (pair + 1) * ROW_TILES)
             out_cols = slice(chunk * SLAB_ROWS, (chunk + 1) * SLAB_ROWS)
 
-            def by_tile(name):
-                return values[chunk, name][:, cols].rearrange("p (t n) -> p t n", n=SLAB_ROWS)
+            def view(place):
+                if place == "cell":
+                    return cell_rows[:, tiles, out_cols]
+                return half(chunk, place[0], int(place[1]), by_tile=True)
 
-            if kind == "cand * i":
-                nc.vector.tensor_tensor(
-                    out=values[chunk, "i"][:, cols],
-                    in0=values[chunk, "i"][:, cols],
-                    in1=values[chunk, "c"][:, cols],
-                    op=ALU.mult,
-                )
-            elif kind == "f * cell":
-                nc.vector.tensor_tensor(
-                    out=by_tile("f"),
-                    in0=by_tile("f"),
-                    in1=cell_rows[:, tiles, out_cols],
-                    op=ALU.mult,
-                )
-            elif kind == "c_new":
-                nc.vector.tensor_tensor(
-                    out=values[chunk, "f"][:, cols],
-                    in0=values[chunk, "f"][:, cols],
-                    in1=values[chunk, "i"][:, cols],
-                    op=ALU.add,
-                )
-                nc.sync.dma_start(out=c_rows[:, tiles, out_cols], in_=by_tile("f"))
-            else:
-                nc.vector.tensor_tensor(
-                    out=values[chunk, "o"][:, cols],
-                    in0=values[chunk, "o"][:, cols],
-                    in1=values[chunk, "tanh_c"][:, cols],
-                    op=ALU.mult,
-                )
-                nc.sync.dma_start(out=h_rows[:, tiles, out_cols], in_=by_tile("o"))
+            out, in0, in1 = [view(place) for place in places]
+            op = ALU.add if kind == "c_new" else ALU.mult
+            engine.tensor_tensor(out=out, in0=in0, in1=in1, op=op)
+            if kind == "c_new":
+                nc.sync.dma_start(out=c_rows[:, tiles, out_cols], in_=out)
+            elif kind == "h_new":
+                nc.sync.dma_start(out=h_rows[:, tiles, out_cols], in_=out)
+
+        SHARED = {
+            "cand * i": (("i0", "i0", "c0"), ("c0", "i1", "c1")),
+            "f * cell": (("c1", "f0", "cell"), ("f0", "f1", "cell")),
+            "c_new": (("c1", "i0", "c1"), ("i0", "c0", "f0")),
+            "h_new": (("o0", "o0", "t0"), ("t0", "o1", "t1")),
+        }
+
+        def combine_shared(chunk, kind):
+            for pair, engine in enumerate((nc.vector, nc.gpsimd)):
+                combine(engine, chunk, kind, pair, SHARED[kind][pair])
 
         order = [("z", 0), ("w", 0), ("z", 1)] + [("w", s) for s in range(1, W_SLABS)]
         raws = {}
@@ -264,12 +266,13 @@ def tile_quest_pa_kernel(
                     const.tile([P, SLAB_WORDS], U8, name="z_scales%d" % pair, align_bytes=64),
                 )
             )
+        in_orders = {}
         mx = {}
         sums = {}
         values = {}
 
-        def turn(slab, in_order=None):
-            grouped = turn_slab(raws[slab], in_order)
+        def turn(slab):
+            grouped = turn_slab(raws[slab], in_orders[slab])
             ahead = order.index(slab) + RAW_BUFS
             if ahead < len(order):
                 raws[order[ahead]] = load_slab(order[ahead])
@@ -285,8 +288,10 @@ def tile_quest_pa_kernel(
                 mx[index] = (codes, scales)
             quantise_slab(grouped, codes, scales)
 
+        sort_slab(order[0])
         for gate, slab in enumerate(order[:4]):
             grouped = turn(slab)
+            sort_slab(order[gate + 1])
             quantise(slab, grouped)
             spread_bias(gate)
             if gate >= 2:
@@ -295,29 +300,41 @@ def tile_quest_pa_kernel(
         kinds = ("cand * i", "f * cell", "c_new", "h_new")
         steps = [(chunk, kind) for chunk in range(CHUNKS) for kind in kinds]
         pairs = (0, 1)
-        in_order = sort_slab(raws["w", FIRST_SORTED])
         for s in range(1, LAST):
-            grouped = turn(("w", s + 1), in_order)
-            for pair in pairs:
-                finish(s - 1, pair)
+            chunk, gate = divmod(s - 1, len(GATES))
+            grouped = turn(("w", s + 1))
             if s >= 3:
-                combine(*steps[s - 3], pairs)
+                combine_shared(*steps[s - 3])
+            for pair in pairs:
+                add_bias(s - 1, pair)
+            if GATES[gate] == "i":
+                squash(chunk, 1)
+            for pair in pairs:
+                activate(s - 1, pair)
+            if GATES[gate] == "c":
+                squash(chunk, 0)
             if s + 2 <= LAST:
-                in_order = sort_slab(raws["w", s + 2])
+                sort_slab(("w", s + 2))
             quantise(("w", s + 1), grouped)
             for pair in pairs:
                 multiply(s, pair)
 
+        last = CHUNKS - 1
+        V, G = nc.vector, nc.gpsimd
+        combine(V, last, "cand * i", 0, ("i0", "i0", "c0"))
+        combine(G, last, "cand * i", 1, ("i1", "i1", "c1"))
         for pair in pairs:
-            finish(LAST - 1, pair)
+            add_bias(LAST - 1, pair)
+            activate(LAST - 1, pair)
         for pair in pairs:
             multiply(LAST, pair)
-        combine(CHUNKS - 1, "cand * i", pairs)
-        finish(LAST, 0)
-        combine(CHUNKS - 1, "f * cell", (0,))
-        combine(CHUNKS - 1, "f * cell", (1,))
-        finish(LAST, 1)
-        combine(CHUNKS - 1, "c_new", (0,))
-        combine(CHUNKS - 1, "h_new", (0,))
-        combine(CHUNKS - 1, "c_new", (1,))
-        combine(CHUNKS - 1, "h_new", (1,))
+        add_bias(LAST, 0)
+        activate(LAST, 0)
+        combine(V, last, "f * cell", 0, ("f0", "f0", "cell"))
+        combine(V, last, "f * cell", 1, ("f1", "f1", "cell"))
+        add_bias(LAST, 1)
+        activate(LAST, 1)
+        combine(V, last, "c_new", 0, ("f0", "f0", "i0"))
+        combine(V, last, "c_new", 1, ("f1", "f1", "i1"))
+        combine(V, last, "h_new", 0, ("o0", "o0", "t0"))
+        combine(V, last, "h_new", 1, ("o1", "o1", "t1"))

@@ -32,12 +32,12 @@ LAST = W_SLABS - 1
 RAW_BUFS = 8
 QUANT_CALLS = 2
 
-SORTED = 3
-BLOCK_WORDS = 16
-RUN = BLOCK_WORDS // 2
+PASS_WORDS = K_PASS // 2
 ROW_WORDS = K // 2
-SORTED_WORDS = SORTED * K_PASS // 2
-PASS_BLOCKS = K_PASS // 32
+SORTED = 3
+HEAD_SORTED = 2
+FIRST_SORTED = 2
+LAST_SORTED = 15
 
 FLOPS = 2 * BATCH * len(GATES) * N_HID * K
 
@@ -80,30 +80,31 @@ def tile_quest_pa_kernel(
                 )
             return raw
 
-        def sort_words(slab, a, passes):
-            first = a * ROW_WORDS + passes[0] * (K_PASS // 2)
-            blocks = slice(passes[0] * PASS_BLOCKS, (passes[-1] + 1) * PASS_BLOCKS)
-            nc.vector.tensor_copy(
-                out=in_orders[slab][a][:].rearrange("p (u b i) -> p u b i", u=2, i=RUN)[:, :, blocks, :],
-                in_=raws[slab][:]
-                .bitcast(F32)[:, first : first + len(passes) * (K_PASS // 2)]
-                .rearrange("p (b u i) -> p u b i", u=2, i=RUN),
-            )
-
         def sort_slab(slab):
-            in_orders[slab] = [
-                sorted_pool.tile([P, SORTED_WORDS], F32, name="in_order%d" % a, tag="in_order%d" % a)
-                for a in range(ROW_TILES)
-            ]
-            if slab[0] == "z":
-                for passes in (range(0, 2), range(2, SORTED)):
-                    for a in range(ROW_TILES):
-                        sort_words(slab, a, passes)
-            else:
-                for a in range(ROW_TILES):
-                    sort_words(slab, a, range(SORTED))
+            in_orders[slab] = []
+            for a in range(ROW_TILES):
+                words = SORTED * PASS_WORDS
+                tile = sorted_pool.tile([P, words], F32, name="in_order%d" % a, tag="in_order%d" % a)
+                nc.vector.tensor_copy(
+                    out=tile[:].rearrange("p (u w) -> p u w", u=2),
+                    in_=raws[slab][:]
+                    .bitcast(F32)[:, a * ROW_WORDS : a * ROW_WORDS + words]
+                    .rearrange("p (w u) -> p u w", u=2),
+                )
+                in_orders[slab].append(tile)
 
-        def turn_slab(raw, in_order):
+        def sort_last_pass(slab):
+            tile = sorted_pool.tile([P, ROW_TILES * PASS_WORDS], F32, name="last_pass", tag="last_pass")
+            nc.scalar.copy(
+                out=tile[:].rearrange("p (a u w) -> p a u w", a=ROW_TILES, u=2),
+                in_=raws[slab][:]
+                .bitcast(F32)
+                .rearrange("p (a w) -> p a w", a=ROW_TILES)[:, :, ROW_WORDS - PASS_WORDS : ROW_WORDS]
+                .rearrange("p a (w u) -> p a u w", u=2),
+            )
+            last_passes[slab] = tile
+
+        def turn_slab(raw, in_order, last_pass):
             raw_words = raw[:].bitcast(F32)
             grouped = grouped_pool.tile(
                 [P, SLAB_WORDS * PACK], BF16, name="grouped", tag="grouped", align_bytes=64
@@ -114,11 +115,14 @@ def tile_quest_pa_kernel(
                 for a in range(ROW_TILES):
                     for u in range(2):
                         place = (2 * a + u) * P
-                        if g < SORTED:
+                        if in_order is not None and g < SORTED:
                             first = (u * SORTED + g) * P
                             words = in_order[a][:, first : first + P]
+                        elif last_pass is not None:
+                            first = (2 * a + u) * P
+                            words = last_pass[:, first : first + P]
                         else:
-                            first = a * ROW_WORDS + g * (K_PASS // 2) + u
+                            first = a * ROW_WORDS + g * PASS_WORDS + u
                             words = raw_words[:, first : first + 2 * P - 1 : 2]
                         nc.tensor.transpose(turned[:, place : place + P], words, ident[:])
                 nc.scalar.copy(
@@ -266,13 +270,14 @@ def tile_quest_pa_kernel(
                     const.tile([P, SLAB_WORDS], U8, name="z_scales%d" % pair, align_bytes=64),
                 )
             )
+        last_passes = {}
         in_orders = {}
         mx = {}
         sums = {}
         values = {}
 
         def turn(slab):
-            grouped = turn_slab(raws[slab], in_orders[slab])
+            grouped = turn_slab(raws[slab], in_orders.get(slab), last_passes.get(slab))
             ahead = order.index(slab) + RAW_BUFS
             if ahead < len(order):
                 raws[order[ahead]] = load_slab(order[ahead])
@@ -288,10 +293,10 @@ def tile_quest_pa_kernel(
                 mx[index] = (codes, scales)
             quantise_slab(grouped, codes, scales)
 
-        sort_slab(order[0])
         for gate, slab in enumerate(order[:4]):
             grouped = turn(slab)
-            sort_slab(order[gate + 1])
+            if gate + 1 >= HEAD_SORTED:
+                sort_slab(order[gate + 1])
             quantise(slab, grouped)
             spread_bias(gate)
             if gate >= 2:
@@ -307,13 +312,13 @@ def tile_quest_pa_kernel(
                 combine_shared(*steps[s - 3])
             for pair in pairs:
                 add_bias(s - 1, pair)
-            if GATES[gate] == "i":
-                squash(chunk, 1)
             for pair in pairs:
                 activate(s - 1, pair)
-            if GATES[gate] == "c":
-                squash(chunk, 0)
-            if s + 2 <= LAST:
+            if GATES[gate] in "ci":
+                squash(chunk, gate)
+            elif s + 2 <= LAST_SORTED:
+                sort_last_pass(("w", s + 2))
+            if FIRST_SORTED <= s + 2 <= LAST_SORTED:
                 sort_slab(("w", s + 2))
             quantise(("w", s + 1), grouped)
             for pair in pairs:
@@ -321,13 +326,13 @@ def tile_quest_pa_kernel(
 
         last = CHUNKS - 1
         V, G = nc.vector, nc.gpsimd
-        combine(V, last, "cand * i", 0, ("i0", "i0", "c0"))
-        combine(G, last, "cand * i", 1, ("i1", "i1", "c1"))
         for pair in pairs:
             add_bias(LAST - 1, pair)
             activate(LAST - 1, pair)
         for pair in pairs:
             multiply(LAST, pair)
+        combine(G, last, "cand * i", 0, ("i0", "i0", "c0"))
+        combine(G, last, "cand * i", 1, ("i1", "i1", "c1"))
         add_bias(LAST, 0)
         activate(LAST, 0)
         combine(V, last, "f * cell", 0, ("f0", "f0", "cell"))
@@ -335,6 +340,6 @@ def tile_quest_pa_kernel(
         add_bias(LAST, 1)
         activate(LAST, 1)
         combine(V, last, "c_new", 0, ("f0", "f0", "i0"))
-        combine(V, last, "c_new", 1, ("f1", "f1", "i1"))
         combine(V, last, "h_new", 0, ("o0", "o0", "t0"))
         combine(V, last, "h_new", 1, ("o1", "o1", "t1"))
+        combine(V, last, "c_new", 1, ("f1", "f1", "i1"))

@@ -34,7 +34,7 @@ QUANT_CALLS = 2
 
 PASS_WORDS = K_PASS // 2
 ROW_WORDS = K // 2
-SORTED = 3
+SORTED = 2
 HEAD_SORTED = 2
 FIRST_SORTED = 2
 LAST_SORTED = 15
@@ -81,30 +81,18 @@ def tile_quest_pa_kernel(
             return raw
 
         def sort_slab(slab):
-            in_orders[slab] = []
-            for a in range(ROW_TILES):
-                words = SORTED * PASS_WORDS
-                tile = sorted_pool.tile([P, words], F32, name="in_order%d" % a, tag="in_order%d" % a)
-                nc.vector.tensor_copy(
-                    out=tile[:].rearrange("p (u w) -> p u w", u=2),
-                    in_=raws[slab][:]
-                    .bitcast(F32)[:, a * ROW_WORDS : a * ROW_WORDS + words]
-                    .rearrange("p (w u) -> p u w", u=2),
-                )
-                in_orders[slab].append(tile)
-
-        def sort_last_pass(slab):
-            tile = sorted_pool.tile([P, ROW_TILES * PASS_WORDS], F32, name="last_pass", tag="last_pass")
-            nc.scalar.copy(
+            words = SORTED * PASS_WORDS
+            tile = sorted_pool.tile([P, ROW_TILES * words], F32, name="in_order", tag="in_order")
+            nc.vector.tensor_copy(
                 out=tile[:].rearrange("p (a u w) -> p a u w", a=ROW_TILES, u=2),
                 in_=raws[slab][:]
                 .bitcast(F32)
-                .rearrange("p (a w) -> p a w", a=ROW_TILES)[:, :, ROW_WORDS - PASS_WORDS : ROW_WORDS]
+                .rearrange("p (a x) -> p a x", a=ROW_TILES)[:, :, 0:words]
                 .rearrange("p a (w u) -> p a u w", u=2),
             )
-            last_passes[slab] = tile
+            in_orders[slab] = tile
 
-        def turn_slab(raw, in_order, last_pass):
+        def turn_slab(raw, in_order):
             raw_words = raw[:].bitcast(F32)
             grouped = grouped_pool.tile(
                 [P, SLAB_WORDS * PACK], BF16, name="grouped", tag="grouped", align_bytes=64
@@ -116,11 +104,8 @@ def tile_quest_pa_kernel(
                     for u in range(2):
                         place = (2 * a + u) * P
                         if in_order is not None and g < SORTED:
-                            first = (u * SORTED + g) * P
-                            words = in_order[a][:, first : first + P]
-                        elif last_pass is not None:
-                            first = (2 * a + u) * P
-                            words = last_pass[:, first : first + P]
+                            first = ((2 * a + u) * SORTED + g) * P
+                            words = in_order[:, first : first + P]
                         else:
                             first = a * ROW_WORDS + g * PASS_WORDS + u
                             words = raw_words[:, first : first + 2 * P - 1 : 2]
@@ -270,14 +255,13 @@ def tile_quest_pa_kernel(
                     const.tile([P, SLAB_WORDS], U8, name="z_scales%d" % pair, align_bytes=64),
                 )
             )
-        last_passes = {}
         in_orders = {}
         mx = {}
         sums = {}
         values = {}
 
         def turn(slab):
-            grouped = turn_slab(raws[slab], in_orders.get(slab), last_passes.get(slab))
+            grouped = turn_slab(raws[slab], in_orders.get(slab))
             ahead = order.index(slab) + RAW_BUFS
             if ahead < len(order):
                 raws[order[ahead]] = load_slab(order[ahead])
@@ -316,8 +300,6 @@ def tile_quest_pa_kernel(
                 activate(s - 1, pair)
             if GATES[gate] in "ci":
                 squash(chunk, gate)
-            elif s + 2 <= LAST_SORTED:
-                sort_last_pass(("w", s + 2))
             if FIRST_SORTED <= s + 2 <= LAST_SORTED:
                 sort_slab(("w", s + 2))
             quantise(("w", s + 1), grouped)
@@ -326,13 +308,13 @@ def tile_quest_pa_kernel(
 
         last = CHUNKS - 1
         V, G = nc.vector, nc.gpsimd
+        combine(V, last, "cand * i", 0, ("i0", "i0", "c0"))
+        combine(G, last, "cand * i", 1, ("i1", "i1", "c1"))
         for pair in pairs:
             add_bias(LAST - 1, pair)
             activate(LAST - 1, pair)
         for pair in pairs:
             multiply(LAST, pair)
-        combine(G, last, "cand * i", 0, ("i0", "i0", "c0"))
-        combine(G, last, "cand * i", 1, ("i1", "i1", "c1"))
         add_bias(LAST, 0)
         activate(LAST, 0)
         combine(V, last, "f * cell", 0, ("f0", "f0", "cell"))
@@ -340,6 +322,6 @@ def tile_quest_pa_kernel(
         add_bias(LAST, 1)
         activate(LAST, 1)
         combine(V, last, "c_new", 0, ("f0", "f0", "i0"))
+        combine(V, last, "c_new", 1, ("f1", "f1", "i1"))
         combine(V, last, "h_new", 0, ("o0", "o0", "t0"))
         combine(V, last, "h_new", 1, ("o1", "o1", "t1"))
-        combine(V, last, "c_new", 1, ("f1", "f1", "i1"))

@@ -29,15 +29,17 @@ CHUNKS = N_HID // SLAB_ROWS
 GATES = ("c", "i", "f", "o")
 W_SLABS = CHUNKS * len(GATES)
 LAST = W_SLABS - 1
+TILES = BATCH // P
+SPLIT = 2
 RAW_BUFS = 8
 QUANT_CALLS = 2
 
 PASS_WORDS = K_PASS // 2
 ROW_WORDS = K // 2
-SORTED = 2
-HEAD_SORTED = 2
+SORTED = 3
+HEAD_SORTED = 3
 FIRST_SORTED = 2
-LAST_SORTED = 15
+LAST_SORTED = 14
 
 FLOPS = 2 * BATCH * len(GATES) * N_HID * K
 
@@ -167,7 +169,7 @@ def tile_quest_pa_kernel(
                 )
             first = gate * N_HID + chunk * SLAB_ROWS
             nc.vector.tensor_tensor(
-                out=half(chunk, name, pair, by_tile=True),
+                out=rows(chunk, name, slice(pair * ROW_TILES, (pair + 1) * ROW_TILES)),
                 in0=sums[s, pair][:].rearrange("p (t n) -> p t n", n=SLAB_ROWS),
                 in1=bias_all[:, first : first + SLAB_ROWS]
                 .unsqueeze(1)
@@ -191,20 +193,18 @@ def tile_quest_pa_kernel(
                 out=half(chunk, "t", pair), in_=half(chunk, "c", pair), func=ACT.Tanh
             )
 
-        def half(chunk, name, place, by_tile=False):
-            view = values[chunk, name][:, place * BANK : (place + 1) * BANK]
-            return view.rearrange("p (t n) -> p t n", n=SLAB_ROWS) if by_tile else view
+        def half(chunk, name, place):
+            return values[chunk, name][:, place * BANK : (place + 1) * BANK]
 
-        def combine(engine, chunk, kind, pair, places):
-            tiles = slice(pair * ROW_TILES, (pair + 1) * ROW_TILES)
+        def rows(chunk, name, tiles):
+            return values[chunk, name][:].rearrange("p (t n) -> p t n", n=SLAB_ROWS)[:, tiles, :]
+
+        def combine(engine, chunk, kind, tiles, operands):
             out_cols = slice(chunk * SLAB_ROWS, (chunk + 1) * SLAB_ROWS)
-
-            def view(place):
-                if place == "cell":
-                    return cell_rows[:, tiles, out_cols]
-                return half(chunk, place[0], int(place[1]), by_tile=True)
-
-            out, in0, in1 = [view(place) for place in places]
+            out, in0, in1 = [
+                cell_rows[:, tiles, out_cols] if name == "cell" else rows(chunk, name, place)
+                for name, place in operands
+            ]
             op = ALU.add if kind == "c_new" else ALU.mult
             engine.tensor_tensor(out=out, in0=in0, in1=in1, op=op)
             if kind == "c_new":
@@ -212,16 +212,18 @@ def tile_quest_pa_kernel(
             elif kind == "h_new":
                 nc.sync.dma_start(out=h_rows[:, tiles, out_cols], in_=out)
 
+        MINE, REST = slice(0, SPLIT), slice(SPLIT, TILES)
+        OVER, FREE = slice(0, TILES - SPLIT), slice(TILES - SPLIT, TILES)
         SHARED = {
-            "cand * i": (("i0", "i0", "c0"), ("c0", "i1", "c1")),
-            "f * cell": (("c1", "f0", "cell"), ("f0", "f1", "cell")),
-            "c_new": (("c1", "i0", "c1"), ("i0", "c0", "f0")),
-            "h_new": (("o0", "o0", "t0"), ("t0", "o1", "t1")),
+            "cand * i": ((("i", MINE), ("i", MINE), ("c", MINE)), (("c", OVER), ("i", REST), ("c", REST))),
+            "f * cell": ((("c", FREE), ("f", MINE), ("cell", MINE)), (("f", OVER), ("f", REST), ("cell", REST))),
+            "c_new": ((("c", FREE), ("i", MINE), ("c", FREE)), (("i", OVER), ("c", OVER), ("f", OVER))),
+            "h_new": ((("o", MINE), ("o", MINE), ("t", MINE)), (("t", OVER), ("o", REST), ("t", REST))),
         }
 
         def combine_shared(chunk, kind):
-            for pair, engine in enumerate((nc.vector, nc.gpsimd)):
-                combine(engine, chunk, kind, pair, SHARED[kind][pair])
+            combine(nc.vector, chunk, kind, MINE, SHARED[kind][0])
+            combine(nc.gpsimd, chunk, kind, REST, SHARED[kind][1])
 
         order = [("z", 0), ("w", 0), ("z", 1)] + [("w", s) for s in range(1, W_SLABS)]
         raws = {}
@@ -308,8 +310,13 @@ def tile_quest_pa_kernel(
 
         last = CHUNKS - 1
         V, G = nc.vector, nc.gpsimd
-        combine(V, last, "cand * i", 0, ("i0", "i0", "c0"))
-        combine(G, last, "cand * i", 1, ("i1", "i1", "c1"))
+        ONE, TWO = slice(0, ROW_TILES), slice(ROW_TILES, TILES)
+
+        def in_place(engine, kind, first, second, tiles):
+            combine(engine, last, kind, tiles, ((first, tiles), (first, tiles), (second, tiles)))
+
+        in_place(V, "cand * i", "i", "c", ONE)
+        in_place(G, "cand * i", "i", "c", TWO)
         for pair in pairs:
             add_bias(LAST - 1, pair)
             activate(LAST - 1, pair)
@@ -317,11 +324,11 @@ def tile_quest_pa_kernel(
             multiply(LAST, pair)
         add_bias(LAST, 0)
         activate(LAST, 0)
-        combine(V, last, "f * cell", 0, ("f0", "f0", "cell"))
-        combine(V, last, "f * cell", 1, ("f1", "f1", "cell"))
+        in_place(V, "f * cell", "f", "cell", ONE)
+        in_place(V, "f * cell", "f", "cell", TWO)
         add_bias(LAST, 1)
         activate(LAST, 1)
-        combine(V, last, "c_new", 0, ("f0", "f0", "i0"))
-        combine(V, last, "c_new", 1, ("f1", "f1", "i1"))
-        combine(V, last, "h_new", 0, ("o0", "o0", "t0"))
-        combine(V, last, "h_new", 1, ("o1", "o1", "t1"))
+        in_place(V, "c_new", "f", "i", ONE)
+        in_place(V, "c_new", "f", "i", TWO)
+        in_place(V, "h_new", "o", "t", ONE)
+        in_place(V, "h_new", "o", "t", TWO)

@@ -30,7 +30,6 @@ GATES = ("c", "i", "f", "o")
 W_SLABS = CHUNKS * len(GATES)
 LAST = W_SLABS - 1
 TILES = BATCH // P
-SPLIT = 2
 RAW_BUFS = 8
 QUANT_CALLS = 2
 
@@ -39,7 +38,7 @@ ROW_WORDS = K // 2
 SORTED = 3
 HEAD_SORTED = 3
 FIRST_SORTED = 2
-LAST_SORTED = 14
+LAST_SORTED = 15
 
 FLOPS = 2 * BATCH * len(GATES) * N_HID * K
 
@@ -169,7 +168,7 @@ def tile_quest_pa_kernel(
                 )
             first = gate * N_HID + chunk * SLAB_ROWS
             nc.vector.tensor_tensor(
-                out=rows(chunk, name, slice(pair * ROW_TILES, (pair + 1) * ROW_TILES)),
+                out=half(chunk, name, pair, by_tile=True),
                 in0=sums[s, pair][:].rearrange("p (t n) -> p t n", n=SLAB_ROWS),
                 in1=bias_all[:, first : first + SLAB_ROWS]
                 .unsqueeze(1)
@@ -193,18 +192,20 @@ def tile_quest_pa_kernel(
                 out=half(chunk, "t", pair), in_=half(chunk, "c", pair), func=ACT.Tanh
             )
 
-        def half(chunk, name, place):
-            return values[chunk, name][:, place * BANK : (place + 1) * BANK]
+        def half(chunk, name, place, by_tile=False):
+            view = values[chunk, name][:, place * BANK : (place + 1) * BANK]
+            return view.rearrange("p (t n) -> p t n", n=SLAB_ROWS) if by_tile else view
 
-        def rows(chunk, name, tiles):
-            return values[chunk, name][:].rearrange("p (t n) -> p t n", n=SLAB_ROWS)[:, tiles, :]
-
-        def combine(engine, chunk, kind, tiles, operands):
+        def combine(engine, chunk, kind, pair, places):
+            tiles = slice(pair * ROW_TILES, (pair + 1) * ROW_TILES)
             out_cols = slice(chunk * SLAB_ROWS, (chunk + 1) * SLAB_ROWS)
-            out, in0, in1 = [
-                cell_rows[:, tiles, out_cols] if name == "cell" else rows(chunk, name, place)
-                for name, place in operands
-            ]
+
+            def view(place):
+                if place == "cell":
+                    return cell_rows[:, tiles, out_cols]
+                return half(chunk, place[0], int(place[1]), by_tile=True)
+
+            out, in0, in1 = [view(place) for place in places]
             op = ALU.add if kind == "c_new" else ALU.mult
             engine.tensor_tensor(out=out, in0=in0, in1=in1, op=op)
             if kind == "c_new":
@@ -212,18 +213,16 @@ def tile_quest_pa_kernel(
             elif kind == "h_new":
                 nc.sync.dma_start(out=h_rows[:, tiles, out_cols], in_=out)
 
-        MINE, REST = slice(0, SPLIT), slice(SPLIT, TILES)
-        OVER, FREE = slice(0, TILES - SPLIT), slice(TILES - SPLIT, TILES)
         SHARED = {
-            "cand * i": ((("i", MINE), ("i", MINE), ("c", MINE)), (("c", OVER), ("i", REST), ("c", REST))),
-            "f * cell": ((("c", FREE), ("f", MINE), ("cell", MINE)), (("f", OVER), ("f", REST), ("cell", REST))),
-            "c_new": ((("c", FREE), ("i", MINE), ("c", FREE)), (("i", OVER), ("c", OVER), ("f", OVER))),
-            "h_new": ((("o", MINE), ("o", MINE), ("t", MINE)), (("t", OVER), ("o", REST), ("t", REST))),
+            "cand * i": (("i0", "i0", "c0"), ("c0", "i1", "c1")),
+            "f * cell": (("c1", "f0", "cell"), ("f0", "f1", "cell")),
+            "c_new": (("c1", "i0", "c1"), ("i0", "c0", "f0")),
+            "h_new": (("o0", "o0", "t0"), ("t0", "o1", "t1")),
         }
 
         def combine_shared(chunk, kind):
-            combine(nc.vector, chunk, kind, MINE, SHARED[kind][0])
-            combine(nc.gpsimd, chunk, kind, REST, SHARED[kind][1])
+            for pair, engine in enumerate((nc.vector, nc.gpsimd)):
+                combine(engine, chunk, kind, pair, SHARED[kind][pair])
 
         order = [("z", 0), ("w", 0), ("z", 1)] + [("w", s) for s in range(1, W_SLABS)]
         raws = {}
@@ -288,47 +287,102 @@ def tile_quest_pa_kernel(
             if gate >= 2:
                 multiply(0, gate - 2)
 
+        bias_cols = const.tile([P, SLAB_ROWS], BF16, name="bias_cols")
+        turned_bias = acc_pool.tile([P, SLAB_ROWS], BF16, name="turned_bias", tag="acc")
+        for j in range(ROW_TILES):
+            first = (CHUNKS - 1) * SLAB_ROWS + j * P
+            nc.tensor.transpose(
+                turned_bias[:, j * P : (j + 1) * P], bias_rows[:, first : first + P], ident_bf[:]
+            )
+        nc.vector.tensor_copy(out=bias_cols[:], in_=turned_bias[:])
+
         kinds = ("cand * i", "f * cell", "c_new", "h_new")
         steps = [(chunk, kind) for chunk in range(CHUNKS) for kind in kinds]
         pairs = (0, 1)
         for s in range(1, LAST):
             chunk, gate = divmod(s - 1, len(GATES))
             grouped = turn(("w", s + 1))
-            if s >= 3:
-                combine_shared(*steps[s - 3])
             for pair in pairs:
                 add_bias(s - 1, pair)
-            for pair in pairs:
-                activate(s - 1, pair)
-            if GATES[gate] in "ci":
-                squash(chunk, gate)
+            if s < LAST - 1:
+                for pair in pairs:
+                    activate(s - 1, pair)
+                if GATES[gate] in "ci":
+                    squash(chunk, gate)
             if FIRST_SORTED <= s + 2 <= LAST_SORTED:
                 sort_slab(("w", s + 2))
+            if s >= 3:
+                combine_shared(*steps[s - 3])
             quantise(("w", s + 1), grouped)
-            for pair in pairs:
-                multiply(s, pair)
+            if s < LAST - 1:
+                for pair in pairs:
+                    multiply(s, pair)
 
         last = CHUNKS - 1
         V, G = nc.vector, nc.gpsimd
-        ONE, TWO = slice(0, ROW_TILES), slice(ROW_TILES, TILES)
+        halves = range(ROW_TILES)
 
-        def in_place(engine, kind, first, second, tiles):
-            combine(engine, last, kind, tiles, ((first, tiles), (first, tiles), (second, tiles)))
+        def multiply_turned(s, j):
+            codes, scales = mx[s]
+            acc = acc_pool.tile([P, BATCH], F32, name="acc", tag="acc")
+            for pair in range(Z_SLABS):
+                for g in range(PASSES):
+                    z_cols = slice(g * SLAB_ROWS, (g + 1) * SLAB_ROWS)
+                    w_cols = slice(g * SLAB_ROWS + j * P, g * SLAB_ROWS + (j + 1) * P)
+                    nc.tensor.matmul_mx(
+                        out=acc[:, pair * SLAB_ROWS : (pair + 1) * SLAB_ROWS],
+                        lhsT=codes[:, w_cols].bitcast(FP8X4),
+                        lhsT_scale=scales[:, w_cols],
+                        rhs=z_mx[pair][0][:, z_cols].bitcast(FP8X4),
+                        rhs_scale=z_mx[pair][1][:, z_cols],
+                        start=(g == 0),
+                        stop=(g == PASSES - 1),
+                    )
+            gate = s % len(GATES)
+            value = gate_pool.tile([P, BATCH], F32, name="turned_gate", tag="turned_gate", bufs=4)
+            nc.scalar.activation(
+                out=value[:],
+                in_=acc[:],
+                func=ACT.Sigmoid,
+                bias=bias_cols[:, j * P + gate : j * P + gate + 1],
+            )
+            return value
 
-        in_place(V, "cand * i", "i", "c", ONE)
-        in_place(G, "cand * i", "i", "c", TWO)
+        def turn_back(value):
+            bank = turn_pool.tile([P, BATCH], F32, name="turned", tag="turned")
+            for t in range(TILES):
+                cols = slice(t * P, (t + 1) * P)
+                nc.tensor.transpose(bank[:, cols], value[:, cols], ident[:])
+            return bank[:].rearrange("p (t n) -> p t n", n=P)
+
+        def columns(name, j):
+            view = values[last, name][:].rearrange("p (t n) -> p t n", n=SLAB_ROWS)
+            return view[:, :, j * P : (j + 1) * P]
+
+        for name in "fo":
+            values[last, name] = gate_pool.tile(
+                [P, Z_SLABS * BANK], F32, name="gate_" + name, tag="gate_" + name
+            )
+        out_cols = [slice(last * SLAB_ROWS + j * P, last * SLAB_ROWS + (j + 1) * P) for j in halves]
         for pair in pairs:
-            add_bias(LAST - 1, pair)
-            activate(LAST - 1, pair)
+            activate(LAST - 2, pair)
+        forget = [multiply_turned(LAST - 1, j) for j in halves]
+        output = [multiply_turned(LAST, 0)]
+        squash(last, 1)
+        combine(V, last, "cand * i", 0, ("i0", "i0", "c0"))
+        combine(V, last, "cand * i", 1, ("i1", "i1", "c1"))
+        for j in halves:
+            nc.vector.tensor_tensor(
+                out=columns("f", j),
+                in0=turn_back(forget[j]),
+                in1=cell_rows[:, :, out_cols[j]],
+                op=ALU.mult,
+            )
+        output.append(multiply_turned(LAST, 1))
         for pair in pairs:
-            multiply(LAST, pair)
-        add_bias(LAST, 0)
-        activate(LAST, 0)
-        in_place(V, "f * cell", "f", "cell", ONE)
-        in_place(V, "f * cell", "f", "cell", TWO)
-        add_bias(LAST, 1)
-        activate(LAST, 1)
-        in_place(V, "c_new", "f", "i", ONE)
-        in_place(V, "c_new", "f", "i", TWO)
-        in_place(V, "h_new", "o", "t", ONE)
-        in_place(V, "h_new", "o", "t", TWO)
+            combine(V, last, "c_new", pair, ("f%d" % pair, "f%d" % pair, "i%d" % pair))
+        for j in halves:
+            nc.vector.tensor_tensor(
+                out=columns("o", j), in0=turn_back(output[j]), in1=columns("t", j), op=ALU.mult
+            )
+            nc.sync.dma_start(out=h_rows[:, :, out_cols[j]], in_=columns("o", j))

@@ -36,6 +36,7 @@ QUANT_CALLS = 2
 PASS_WORDS = K_PASS // 2
 ROW_WORDS = K // 2
 SORTED = 3
+FULLY_SORTED = 8
 HEAD_SORTED = 3
 FIRST_SORTED = 2
 LAST_SORTED = 15
@@ -82,7 +83,8 @@ def tile_quest_pa_kernel(
             return raw
 
         def sort_slab(slab):
-            words = SORTED * PASS_WORDS
+            passes = PASSES if slab[1] < FULLY_SORTED else SORTED
+            words = passes * PASS_WORDS
             tile = sorted_pool.tile([P, ROW_TILES * words], F32, name="in_order", tag="in_order")
             nc.vector.tensor_copy(
                 out=tile[:].rearrange("p (a u w) -> p a u w", a=ROW_TILES, u=2),
@@ -91,9 +93,10 @@ def tile_quest_pa_kernel(
                 .rearrange("p (a x) -> p a x", a=ROW_TILES)[:, :, 0:words]
                 .rearrange("p a (w u) -> p a u w", u=2),
             )
-            in_orders[slab] = tile
+            in_orders[slab] = (tile, passes)
 
         def turn_slab(raw, in_order):
+            in_order, passes = in_order
             raw_words = raw[:].bitcast(F32)
             grouped = grouped_pool.tile(
                 [P, SLAB_WORDS * PACK], BF16, name="grouped", tag="grouped", align_bytes=64
@@ -104,8 +107,8 @@ def tile_quest_pa_kernel(
                 for a in range(ROW_TILES):
                     for u in range(2):
                         place = (2 * a + u) * P
-                        if in_order is not None and g < SORTED:
-                            first = ((2 * a + u) * SORTED + g) * P
+                        if g < passes:
+                            first = ((2 * a + u) * passes + g) * P
                             words = in_order[:, first : first + P]
                         else:
                             first = a * ROW_WORDS + g * PASS_WORDS + u
@@ -130,8 +133,9 @@ def tile_quest_pa_kernel(
 
         def spread_bias(gate):
             spread = acc_pool.tile([P, N_HID], BF16, name="spread", tag="acc")
-            for half in range(N_HID // BANK):
-                cols = slice(half * BANK, (half + 1) * BANK)
+            width = N_HID if GATES[gate] in "ci" else (CHUNKS - 1) * SLAB_ROWS
+            for first in range(0, width, BANK):
+                cols = slice(first, min(first + BANK, width))
                 nc.tensor.matmul(
                     out=spread[:, cols],
                     lhsT=ident_bf[:, gate : gate + 1].to_broadcast([P, P]),
@@ -139,7 +143,14 @@ def tile_quest_pa_kernel(
                     start=True,
                     stop=True,
                 )
-            nc.vector.tensor_copy(out=bias_all[:, gate * N_HID : (gate + 1) * N_HID], in_=spread[:])
+            if gate == len(GATES) - 1:
+                for j in range(ROW_TILES):
+                    cols = slice(width + j * P, width + (j + 1) * P)
+                    nc.tensor.transpose(spread[:, cols], bias_rows[:, cols], ident_bf[:])
+                width = N_HID
+            nc.vector.tensor_copy(
+                out=bias_all[:, gate * N_HID : gate * N_HID + width], in_=spread[:, 0:width]
+            )
 
         def multiply(s, pair):
             codes, scales = mx[s]
@@ -244,6 +255,7 @@ def tile_quest_pa_kernel(
         ident_bf = const.tile([P, P], BF16, name="ident_bf")
         nc.vector.tensor_copy(out=ident_bf[:], in_=ident[:])
         bias_all = const.tile([P, len(GATES) * N_HID], BF16, name="bias_all")
+        bias_cols = bias_all[:, len(GATES) * N_HID - SLAB_ROWS : len(GATES) * N_HID]
         warm = const.tile([P, 1], F32, name="warm")
         nc.vector.memset(warm[:], 0.0)
         nc.scalar.activation(out=warm[:], in_=warm[:], func=ACT.Sigmoid)
@@ -262,7 +274,7 @@ def tile_quest_pa_kernel(
         values = {}
 
         def turn(slab):
-            grouped = turn_slab(raws[slab], in_orders.get(slab))
+            grouped = turn_slab(raws[slab], in_orders.get(slab, (None, 0)))
             ahead = order.index(slab) + RAW_BUFS
             if ahead < len(order):
                 raws[order[ahead]] = load_slab(order[ahead])
@@ -287,15 +299,6 @@ def tile_quest_pa_kernel(
             if gate >= 2:
                 multiply(0, gate - 2)
 
-        bias_cols = const.tile([P, SLAB_ROWS], BF16, name="bias_cols")
-        turned_bias = acc_pool.tile([P, SLAB_ROWS], BF16, name="turned_bias", tag="acc")
-        for j in range(ROW_TILES):
-            first = (CHUNKS - 1) * SLAB_ROWS + j * P
-            nc.tensor.transpose(
-                turned_bias[:, j * P : (j + 1) * P], bias_rows[:, first : first + P], ident_bf[:]
-            )
-        nc.vector.tensor_copy(out=bias_cols[:], in_=turned_bias[:])
-
         kinds = ("cand * i", "f * cell", "c_new", "h_new")
         steps = [(chunk, kind) for chunk in range(CHUNKS) for kind in kinds]
         pairs = (0, 1)
@@ -311,7 +314,7 @@ def tile_quest_pa_kernel(
                     squash(chunk, gate)
             if FIRST_SORTED <= s + 2 <= LAST_SORTED:
                 sort_slab(("w", s + 2))
-            if s >= 3:
+            if 3 <= s < LAST - 1:
                 combine_shared(*steps[s - 3])
             quantise(("w", s + 1), grouped)
             if s < LAST - 1:
@@ -322,15 +325,16 @@ def tile_quest_pa_kernel(
         V, G = nc.vector, nc.gpsimd
         halves = range(ROW_TILES)
 
-        def multiply_turned(s, j):
+        def multiply_turned(s, j, slabs):
             codes, scales = mx[s]
-            acc = acc_pool.tile([P, BATCH], F32, name="acc", tag="acc")
-            for pair in range(Z_SLABS):
+            width = len(slabs) * SLAB_ROWS
+            acc = acc_pool.tile([P, width], F32, name="acc", tag="acc")
+            for place, pair in enumerate(slabs):
                 for g in range(PASSES):
                     z_cols = slice(g * SLAB_ROWS, (g + 1) * SLAB_ROWS)
                     w_cols = slice(g * SLAB_ROWS + j * P, g * SLAB_ROWS + (j + 1) * P)
                     nc.tensor.matmul_mx(
-                        out=acc[:, pair * SLAB_ROWS : (pair + 1) * SLAB_ROWS],
+                        out=acc[:, place * SLAB_ROWS : (place + 1) * SLAB_ROWS],
                         lhsT=codes[:, w_cols].bitcast(FP8X4),
                         lhsT_scale=scales[:, w_cols],
                         rhs=z_mx[pair][0][:, z_cols].bitcast(FP8X4),
@@ -339,7 +343,7 @@ def tile_quest_pa_kernel(
                         stop=(g == PASSES - 1),
                     )
             gate = s % len(GATES)
-            value = gate_pool.tile([P, BATCH], F32, name="turned_gate", tag="turned_gate", bufs=4)
+            value = gate_pool.tile([P, width], F32, name="turned_gate", tag="turned_gate", bufs=5)
             nc.scalar.activation(
                 out=value[:],
                 in_=acc[:],
@@ -348,17 +352,19 @@ def tile_quest_pa_kernel(
             )
             return value
 
-        def turn_back(value):
-            bank = turn_pool.tile([P, BATCH], F32, name="turned", tag="turned")
-            for t in range(TILES):
+        def turn_back(value, slabs):
+            bank = turn_pool.tile([P, len(slabs) * SLAB_ROWS], F32, name="turned", tag="turned")
+            for t in range(len(slabs) * ROW_TILES):
                 cols = slice(t * P, (t + 1) * P)
                 nc.tensor.transpose(bank[:, cols], value[:, cols], ident[:])
             return bank[:].rearrange("p (t n) -> p t n", n=P)
 
-        def columns(name, j):
+        def columns(name, j, slabs):
             view = values[last, name][:].rearrange("p (t n) -> p t n", n=SLAB_ROWS)
-            return view[:, :, j * P : (j + 1) * P]
+            tiles = slice(slabs[0] * ROW_TILES, (slabs[-1] + 1) * ROW_TILES)
+            return view[:, tiles, j * P : (j + 1) * P]
 
+        combine_shared(*steps[LAST - 4])
         for name in "fo":
             values[last, name] = gate_pool.tile(
                 [P, Z_SLABS * BANK], F32, name="gate_" + name, tag="gate_" + name
@@ -366,23 +372,29 @@ def tile_quest_pa_kernel(
         out_cols = [slice(last * SLAB_ROWS + j * P, last * SLAB_ROWS + (j + 1) * P) for j in halves]
         for pair in pairs:
             activate(LAST - 2, pair)
-        forget = [multiply_turned(LAST - 1, j) for j in halves]
-        output = [multiply_turned(LAST, 0)]
+        forget = [multiply_turned(LAST - 1, j, pairs) for j in halves]
+        first_output = multiply_turned(LAST, 0, pairs)
         squash(last, 1)
-        combine(V, last, "cand * i", 0, ("i0", "i0", "c0"))
-        combine(V, last, "cand * i", 1, ("i1", "i1", "c1"))
+        for pair in pairs:
+            i, c = "i%d" % pair, "c%d" % pair
+            combine(V, last, "cand * i", pair, (i, i, c))
         for j in halves:
             nc.vector.tensor_tensor(
-                out=columns("f", j),
-                in0=turn_back(forget[j]),
+                out=columns("f", j, pairs),
+                in0=turn_back(forget[j], pairs),
                 in1=cell_rows[:, :, out_cols[j]],
                 op=ALU.mult,
             )
-        output.append(multiply_turned(LAST, 1))
+        last_outputs = [(slabs, multiply_turned(LAST, 1, slabs)) for slabs in ((0,), (1,))]
         for pair in pairs:
-            combine(V, last, "c_new", pair, ("f%d" % pair, "f%d" % pair, "i%d" % pair))
-        for j in halves:
+            f, i = "f%d" % pair, "i%d" % pair
+            combine(V, last, "c_new", pair, (f, f, i))
+        for j, slabs, value in [(0, pairs, first_output)] + [(1,) + each for each in last_outputs]:
             nc.vector.tensor_tensor(
-                out=columns("o", j), in0=turn_back(output[j]), in1=columns("t", j), op=ALU.mult
+                out=columns("o", j, slabs),
+                in0=turn_back(value, slabs),
+                in1=columns("t", j, slabs),
+                op=ALU.mult,
             )
-            nc.sync.dma_start(out=h_rows[:, :, out_cols[j]], in_=columns("o", j))
+            tiles = slice(slabs[0] * ROW_TILES, (slabs[-1] + 1) * ROW_TILES)
+            nc.sync.dma_start(out=h_rows[:, tiles, out_cols[j]], in_=columns("o", j, slabs))

from contextlib import ExitStack

import concourse.mybir as mybir
from concourse.masks import make_identity

FP8X4 = mybir.dt.float8_e4m3fn_x4
BF16 = mybir.dt.bfloat16
F32 = mybir.dt.float32
U32 = mybir.dt.uint32
U8 = mybir.dt.uint8
ACT = mybir.ActivationFunctionType
ALU = mybir.AluOpType

P = 128
BATCH = 512
N_IN = 1024
N_HID = 1024
K = N_IN + N_HID
PACK = 4
K_PASS = P * PACK
PASSES = K // K_PASS
BANK = 512

SLAB_ROWS = 256
ROW_TILES = SLAB_ROWS // P
SLAB_WORDS = PASSES * SLAB_ROWS
Z_SLABS = BATCH // SLAB_ROWS
CHUNKS = N_HID // SLAB_ROWS
GATES = ("c", "i", "f", "o")
W_SLABS = CHUNKS * len(GATES)
LAST = W_SLABS - 1
TILES = BATCH // P
RAW_BUFS = 8
QUANT_CALLS = 2

PASS_WORDS = K_PASS // 2
ROW_WORDS = K // 2
SORTED = 3
FULLY_SORTED = 8
HEAD_SORTED = 3
FIRST_SORTED = 2
LAST_SORTED = 15

FLOPS = 2 * BATCH * len(GATES) * N_HID * K


def tile_quest_pa_kernel(
    tc, X, hidden1, cell1, Wf1, bf1, Wi1, bi1, Wc1, bc1, Wo1, bo1, out_0, out_1
):
    nc = tc.nc
    weight = {"f": Wf1, "i": Wi1, "c": Wc1, "o": Wo1}
    bias = {"f": bf1, "i": bi1, "c": bc1, "o": bo1}
    h_rows = out_0.rearrange("(t p) n -> p t n", p=P)
    c_rows = out_1.rearrange("(t p) n -> p t n", p=P)

    with ExitStack() as ctx:
        const = ctx.enter_context(tc.tile_pool(name="const", bufs=1))
        raw_pool = ctx.enter_context(tc.tile_pool(name="raw", bufs=RAW_BUFS))
        sorted_pool = ctx.enter_context(tc.tile_pool(name="sorted", bufs=2))
        grouped_pool = ctx.enter_context(tc.tile_pool(name="grouped", bufs=2))
        w_pool = ctx.enter_context(tc.tile_pool(name="w_mx", bufs=3))
        gate_pool = ctx.enter_context(tc.tile_pool(name="gates", bufs=2))
        turn_pool = ctx.enter_context(tc.psum_pool(name="turned", bufs=4))
        acc_pool = ctx.enter_context(tc.psum_pool(name="acc", bufs=4))
        ctx.enter_context(tc.manual_schedule())

        def load_slab(slab):
            kind, index = slab
            raw = raw_pool.tile([P, ROW_TILES * K], BF16, name="raw", tag="raw")
            raw_rows = raw[:].rearrange("p (a k) -> p a k", a=ROW_TILES)
            if kind == "z":
                for source, cols in ((X, slice(0, N_IN)), (hidden1, slice(N_IN, K))):
                    for a in range(ROW_TILES):
                        first = index * SLAB_ROWS + a * P
                        nc.sync.dma_start(out=raw_rows[:, a, cols], in_=source[first : first + P, :])
            else:
                chunk, gate = divmod(index, len(GATES))
                rows = slice(chunk * SLAB_ROWS, (chunk + 1) * SLAB_ROWS)
                nc.sync.dma_start(
                    out=raw_rows,
                    in_=weight[GATES[gate]][rows, :].rearrange("(a p) k -> p a k", p=P),
                )
            return raw

        def sort_slab(slab):
            passes = PASSES if slab[1] < FULLY_SORTED else SORTED
            words = passes * PASS_WORDS
            tile = sorted_pool.tile([P, ROW_TILES * words], F32, name="in_order", tag="in_order")
            nc.vector.tensor_copy(
                out=tile[:].rearrange("p (a u w) -> p a u w", a=ROW_TILES, u=2),
                in_=raws[slab][:]
                .bitcast(F32)
                .rearrange("p (a x) -> p a x", a=ROW_TILES)[:, :, 0:words]
                .rearrange("p a (w u) -> p a u w", u=2),
            )
            in_orders[slab] = (tile, passes)

        def turn_slab(raw, in_order):
            in_order, passes = in_order
            raw_words = raw[:].bitcast(F32)
            grouped = grouped_pool.tile(
                [P, SLAB_WORDS * PACK], BF16, name="grouped", tag="grouped", align_bytes=64
            )
            grouped_words = grouped[:].bitcast(F32)
            for g in range(PASSES):
                turned = turn_pool.tile([P, BANK], F32, name="turned", tag="turned")
                for a in range(ROW_TILES):
                    for u in range(2):
                        place = (2 * a + u) * P
                        if g < passes:
                            first = ((2 * a + u) * passes + g) * P
                            words = in_order[:, first : first + P]
                        else:
                            first = a * ROW_WORDS + g * PASS_WORDS + u
                            words = raw_words[:, first : first + 2 * P - 1 : 2]
                        nc.tensor.transpose(turned[:, place : place + P], words, ident[:])
                nc.scalar.copy(
                    out=grouped_words[:, g * BANK : (g + 1) * BANK].rearrange(
                        "p (a r u) -> p a r u", a=ROW_TILES, u=2
                    ),
                    in_=turned[:].rearrange("p (a u r) -> p a r u", a=ROW_TILES, u=2),
                )
            return grouped

        def quantise_slab(grouped, codes, scales):
            words = SLAB_WORDS // QUANT_CALLS
            for call in range(QUANT_CALLS):
                nc.vector.quantize_mx(
                    out=codes[:, call * words : (call + 1) * words].bitcast(FP8X4),
                    scales=scales[:, call * words : (call + 1) * words],
                    in_=grouped[:, call * words * PACK : (call + 1) * words * PACK],
                )

        def spread_bias(gate):
            spread = acc_pool.tile([P, N_HID], BF16, name="spread", tag="acc")
            width = N_HID if GATES[gate] in "ci" else (CHUNKS - 1) * SLAB_ROWS
            for first in range(0, width, BANK):
                cols = slice(first, min(first + BANK, width))
                nc.tensor.matmul(
                    out=spread[:, cols],
                    lhsT=ident_bf[:, gate : gate + 1].to_broadcast([P, P]),
                    rhs=bias_rows[:, cols],
                    start=True,
                    stop=True,
                )
            if gate == len(GATES) - 1:
                for j in range(ROW_TILES):
                    cols = slice(width + j * P, width + (j + 1) * P)
                    nc.tensor.transpose(spread[:, cols], bias_rows[:, cols], ident_bf[:])
                width = N_HID
            nc.vector.tensor_copy(
                out=bias_all[:, gate * N_HID : gate * N_HID + width], in_=spread[:, 0:width]
            )

        def multiply(s, pair):
            codes, scales = mx[s]
            acc = acc_pool.tile([P, BANK], F32, name="acc", tag="acc")
            for a in range(ROW_TILES):
                for g in range(PASSES):
                    z_cols = slice(g * SLAB_ROWS + a * P, g * SLAB_ROWS + (a + 1) * P)
                    w_cols = slice(g * SLAB_ROWS, (g + 1) * SLAB_ROWS)
                    nc.tensor.matmul_mx(
                        out=acc[:, a * SLAB_ROWS : (a + 1) * SLAB_ROWS],
                        lhsT=z_mx[pair][0][:, z_cols].bitcast(FP8X4),
                        lhsT_scale=z_mx[pair][1][:, z_cols],
                        rhs=codes[:, w_cols].bitcast(FP8X4),
                        rhs_scale=scales[:, w_cols],
                        start=(g == 0),
                        stop=(g == PASSES - 1),
                    )
            sums[s, pair] = acc

        def add_bias(s, pair):
            chunk, gate = divmod(s, len(GATES))
            name = GATES[gate]
            if pair == 0:
                values[chunk, name] = gate_pool.tile(
                    [P, Z_SLABS * BANK], F32, name="gate_" + name, tag="gate_" + name
                )
            first = gate * N_HID + chunk * SLAB_ROWS
            nc.vector.tensor_tensor(
                out=half(chunk, name, pair, by_tile=True),
                in0=sums[s, pair][:].rearrange("p (t n) -> p t n", n=SLAB_ROWS),
                in1=bias_all[:, first : first + SLAB_ROWS]
                .unsqueeze(1)
                .to_broadcast([P, ROW_TILES, SLAB_ROWS]),
                op=ALU.add,
            )

        def activate(s, pair):
            chunk, gate = divmod(s, len(GATES))
            value = half(chunk, GATES[gate], pair)
            nc.scalar.activation(
                out=value, in_=value, func=ACT.Tanh if GATES[gate] == "c" else ACT.Sigmoid
            )

        def squash(chunk, pair):
            if pair == 0:
                values[chunk, "t"] = gate_pool.tile(
                    [P, Z_SLABS * BANK], F32, name="t", tag="t"
                )
            nc.scalar.activation(
                out=half(chunk, "t", pair), in_=half(chunk, "c", pair), func=ACT.Tanh
            )

        def half(chunk, name, place, by_tile=False):
            view = values[chunk, name][:, place * BANK : (place + 1) * BANK]
            return view.rearrange("p (t n) -> p t n", n=SLAB_ROWS) if by_tile else view

        def combine(engine, chunk, kind, pair, places):
            tiles = slice(pair * ROW_TILES, (pair + 1) * ROW_TILES)
            out_cols = slice(chunk * SLAB_ROWS, (chunk + 1) * SLAB_ROWS)

            def view(place):
                if place == "cell":
                    return cell_rows[:, tiles, out_cols]
                return half(chunk, place[0], int(place[1]), by_tile=True)

            out, in0, in1 = [view(place) for place in places]
            op = ALU.add if kind == "c_new" else ALU.mult
            engine.tensor_tensor(out=out, in0=in0, in1=in1, op=op)
            if kind == "c_new":
                nc.sync.dma_start(out=c_rows[:, tiles, out_cols], in_=out)
            elif kind == "h_new":
                nc.sync.dma_start(out=h_rows[:, tiles, out_cols], in_=out)

        SHARED = {
            "cand * i": (("i0", "i0", "c0"), ("c0", "i1", "c1")),
            "f * cell": (("c1", "f0", "cell"), ("f0", "f1", "cell")),
            "c_new": (("c1", "i0", "c1"), ("i0", "c0", "f0")),
            "h_new": (("o0", "o0", "t0"), ("t0", "o1", "t1")),
        }

        def combine_shared(chunk, kind):
            for pair, engine in enumerate((nc.vector, nc.gpsimd)):
                combine(engine, chunk, kind, pair, SHARED[kind][pair])

        order = [("z", 0), ("w", 0), ("z", 1)] + [("w", s) for s in range(1, W_SLABS)]
        raws = {}
        for slab in order[:RAW_BUFS]:
            raws[slab] = load_slab(slab)
        cell_sb = const.tile([P, (BATCH // P) * N_HID], BF16, name="cell_sb")
        cell_rows = cell_sb[:].rearrange("p (t n) -> p t n", n=N_HID)
        nc.sync.dma_start(out=cell_rows, in_=cell1.rearrange("(t p) n -> p t n", p=P))

        bias_rows = const.tile([P, N_HID], BF16, name="bias_rows")
        nc.vector.memset(bias_rows[:].bitcast(F32), 0.0)
        for gate in range(len(GATES)):
            nc.scalar.dma_start(
                out=bias_rows[gate : gate + 1, :],
                in_=bias[GATES[gate]].rearrange("(o n) -> o n", o=1),
            )
        ident = const.tile([P, P], F32, name="ident")
        make_identity(nc, ident[:])
        ident_bf = const.tile([P, P], BF16, name="ident_bf")
        nc.vector.tensor_copy(out=ident_bf[:], in_=ident[:])
        bias_all = const.tile([P, len(GATES) * N_HID], BF16, name="bias_all")
        bias_cols = bias_all[:, len(GATES) * N_HID - SLAB_ROWS : len(GATES) * N_HID]
        warm = const.tile([P, 1], F32, name="warm")
        nc.vector.memset(warm[:], 0.0)
        nc.scalar.activation(out=warm[:], in_=warm[:], func=ACT.Sigmoid)

        z_mx = []
        for pair in range(Z_SLABS):
            z_mx.append(
                (
                    const.tile([P, SLAB_WORDS], U32, name="z_codes%d" % pair, align_bytes=64),
                    const.tile([P, SLAB_WORDS], U8, name="z_scales%d" % pair, align_bytes=64),
                )
            )
        in_orders = {}
        mx = {}
        sums = {}
        values = {}

        def turn(slab):
            grouped = turn_slab(raws[slab], in_orders.get(slab, (None, 0)))
            ahead = order.index(slab) + RAW_BUFS
            if ahead < len(order):
                raws[order[ahead]] = load_slab(order[ahead])
            return grouped

        def quantise(slab, grouped):
            kind, index = slab
            if kind == "z":
                codes, scales = z_mx[index]
            else:
                codes = w_pool.tile([P, SLAB_WORDS], U32, name="codes", tag="codes", align_bytes=64)
                scales = w_pool.tile([P, SLAB_WORDS], U8, name="scales", tag="scales", align_bytes=64)
                mx[index] = (codes, scales)
            quantise_slab(grouped, codes, scales)

        for gate, slab in enumerate(order[:4]):
            grouped = turn(slab)
            if gate + 1 >= HEAD_SORTED:
                sort_slab(order[gate + 1])
            quantise(slab, grouped)
            spread_bias(gate)
            if gate >= 2:
                multiply(0, gate - 2)

        kinds = ("cand * i", "f * cell", "c_new", "h_new")
        steps = [(chunk, kind) for chunk in range(CHUNKS) for kind in kinds]
        pairs = (0, 1)
        for s in range(1, LAST):
            chunk, gate = divmod(s - 1, len(GATES))
            grouped = turn(("w", s + 1))
            for pair in pairs:
                add_bias(s - 1, pair)
            if s < LAST - 1:
                for pair in pairs:
                    activate(s - 1, pair)
                if GATES[gate] in "ci":
                    squash(chunk, gate)
            if FIRST_SORTED <= s + 2 <= LAST_SORTED:
                sort_slab(("w", s + 2))
            if 3 <= s < LAST - 1:
                combine_shared(*steps[s - 3])
            quantise(("w", s + 1), grouped)
            if s < LAST - 1:
                for pair in pairs:
                    multiply(s, pair)

        last = CHUNKS - 1
        V, G = nc.vector, nc.gpsimd
        halves = range(ROW_TILES)

        def multiply_turned(s, j, slabs):
            codes, scales = mx[s]
            width = len(slabs) * SLAB_ROWS
            acc = acc_pool.tile([P, width], F32, name="acc", tag="acc")
            for place, pair in enumerate(slabs):
                for g in range(PASSES):
                    z_cols = slice(g * SLAB_ROWS, (g + 1) * SLAB_ROWS)
                    w_cols = slice(g * SLAB_ROWS + j * P, g * SLAB_ROWS + (j + 1) * P)
                    nc.tensor.matmul_mx(
                        out=acc[:, place * SLAB_ROWS : (place + 1) * SLAB_ROWS],
                        lhsT=codes[:, w_cols].bitcast(FP8X4),
                        lhsT_scale=scales[:, w_cols],
                        rhs=z_mx[pair][0][:, z_cols].bitcast(FP8X4),
                        rhs_scale=z_mx[pair][1][:, z_cols],
                        start=(g == 0),
                        stop=(g == PASSES - 1),
                    )
            gate = s % len(GATES)
            value = gate_pool.tile([P, width], F32, name="turned_gate", tag="turned_gate", bufs=5)
            nc.scalar.activation(
                out=value[:],
                in_=acc[:],
                func=ACT.Sigmoid,
                bias=bias_cols[:, j * P + gate : j * P + gate + 1],
            )
            return value

        def turn_back(value, slabs):
            bank = turn_pool.tile([P, len(slabs) * SLAB_ROWS], F32, name="turned", tag="turned")
            for t in range(len(slabs) * ROW_TILES):
                cols = slice(t * P, (t + 1) * P)
                nc.tensor.transpose(bank[:, cols], value[:, cols], ident[:])
            return bank[:].rearrange("p (t n) -> p t n", n=P)

        def columns(name, j, slabs):
            view = values[last, name][:].rearrange("p (t n) -> p t n", n=SLAB_ROWS)
            tiles = slice(slabs[0] * ROW_TILES, (slabs[-1] + 1) * ROW_TILES)
            return view[:, tiles, j * P : (j + 1) * P]

        combine_shared(*steps[LAST - 4])
        for name in "fo":
            values[last, name] = gate_pool.tile(
                [P, Z_SLABS * BANK], F32, name="gate_" + name, tag="gate_" + name
            )
        out_cols = [slice(last * SLAB_ROWS + j * P, last * SLAB_ROWS + (j + 1) * P) for j in halves]
        for pair in pairs:
            activate(LAST - 2, pair)
        forget = [multiply_turned(LAST - 1, j, pairs) for j in halves]
        first_output = multiply_turned(LAST, 0, pairs)
        squash(last, 1)
        for pair in pairs:
            i, c = "i%d" % pair, "c%d" % pair
            combine(V, last, "cand * i", pair, (i, i, c))
        for j in halves:
            nc.vector.tensor_tensor(
                out=columns("f", j, pairs),
                in0=turn_back(forget[j], pairs),
                in1=cell_rows[:, :, out_cols[j]],
                op=ALU.mult,
            )
        last_outputs = [(slabs, multiply_turned(LAST, 1, slabs)) for slabs in ((0,), (1,))]
        for pair in pairs:
            f, i = "f%d" % pair, "i%d" % pair
            combine(V, last, "c_new", pair, (f, f, i))
        for j, slabs, value in [(0, pairs, first_output)] + [(1,) + each for each in last_outputs]:
            nc.vector.tensor_tensor(
                out=columns("o", j, slabs),
                in0=turn_back(value, slabs),
                in1=columns("t", j, slabs),
                op=ALU.mult,
            )
            tiles = slice(slabs[0] * ROW_TILES, (slabs[-1] + 1) * ROW_TILES)
            nc.sync.dma_start(out=h_rows[:, tiles, out_cols[j]], in_=columns("o", j, slabs))
